import numpy as np
import ml_dtypes


def mxq(x, axis, fmt="e4m3"):
    dtype, down = {"e4m3": (ml_dtypes.float8_e4m3fn, 7), "e5m2": (ml_dtypes.float8_e5m2, 14)}[fmt]
    v = np.moveaxis(np.asarray(x, np.float32).astype(ml_dtypes.bfloat16).astype(np.float64), axis, -1)
    blocks = v.reshape(v.shape[:-1] + (-1, 32))
    amax = np.abs(blocks).max(-1, keepdims=True)
    byte = np.maximum(np.where(amax > 0, np.frexp(amax)[1] - 1 + 127, 0) - down, 1)
    scale = np.exp2(byte - 127.0)
    codes = (blocks / scale).astype(np.float32).astype(dtype).astype(np.float64)
    return np.moveaxis((codes * scale).reshape(v.shape), -1, axis)


WIDE = False


def mx_kscale(k):
    if not WIDE:
        return np.ones(k)
    levels = np.array([10, -10, 5, -5, 0])
    a = np.random.permutation(np.resize(levels, k // 512 * 4)).reshape(k // 512, 4)
    idx = np.arange(k)
    return np.exp2(a[idx // 512, idx % 128 // 32])


BF16 = ml_dtypes.bfloat16


def bf(x):
    return np.asarray(x, np.float32).astype(BF16)


def f64(x):
    return np.asarray(x).astype(np.float64)


E2M1 = np.array([0.0, 0.5, 1.0, 1.5, 2.0, 3.0, 4.0, 6.0, -0.0, -0.5, -1.0, -1.5, -2.0, -3.0, -4.0, -6.0])


def pack_weight(w, fmt):
    k, n = w.shape
    w = f64(bf(w)).reshape(k // 32, 32, n)
    amax = np.abs(w).max(1)
    if fmt == "e4m3":
        byte = np.frexp(amax)[1] - 1 + 127 - 7
    else:
        mant, ex = np.frexp(amax / 6.0)
        byte = np.where(mant > 0.5, ex, ex - 1) + 127
    byte = np.clip(np.where(amax > 0, byte, 1), 1, 254)
    scaled = (w * np.exp2(127.0 - byte)[:, None, :]).reshape(k, n).astype(np.float32)
    by_word = np.ascontiguousarray(scaled.reshape(k // 512, 128, 4, n).transpose(0, 1, 3, 2))
    if fmt == "e4m3":
        words = by_word.astype(ml_dtypes.float8_e4m3fn).view(np.uint8)
    else:
        c = by_word.astype(ml_dtypes.float4_e2m1fn).view(np.uint8) & 0xF
        words = c[..., 0::2] | (c[..., 1::2] << 4)
    return np.ascontiguousarray(words), np.ascontiguousarray(byte.astype(np.uint8).reshape(k // 512, 16, n))


def unpack_weight(words, scales, fmt):
    g, p, n, _ = words.shape
    if fmt == "e4m3":
        vals = np.ascontiguousarray(words).view(ml_dtypes.float8_e4m3fn).astype(np.float64)
    else:
        nib = np.empty((g, p, n, 4), np.uint8)
        nib[..., 0::2] = words & 0xF
        nib[..., 1::2] = words >> 4
        vals = E2M1[nib]
    vals = vals * np.repeat(np.exp2(scales.astype(np.float64) - 127.0), 8, axis=1)[..., None]
    return vals.transpose(0, 1, 3, 2).reshape(g * 512, n)


B, N, NF, ND, NH = 16, 8, 512, 8192, 512


def setup_inputs():
    s = mx_kscale(ND)
    t = mx_kscale(NH)
    atom_features = bf(np.random.standard_normal((B, N, NF)))
    distance_matrix = bf(np.random.random((B, N, N, ND)) * s)
    distance_matrix_mask = bf(0.25 + 0.75 * np.random.random((B, N, N)))
    W_cf = bf(np.random.standard_normal((NF, NH)) / np.sqrt(NF) * t)
    W_df_words, W_df_scales = pack_weight(np.random.standard_normal((ND, NH)) * 1.5 / np.sqrt(ND) / s[:, None], "e4m3")
    W_fc_words, W_fc_scales = pack_weight(np.random.standard_normal((NH, NF)) / np.sqrt(NH) / t[:, None], "e4m3")
    b_cf = bf(np.random.standard_normal(NH) * 0.3 * t)
    b_df = bf(np.random.standard_normal(NH) * 0.3)
    return {
        "atom_features": atom_features,
        "distance_matrix": distance_matrix,
        "distance_matrix_mask": distance_matrix_mask,
        "W_cf": W_cf,
        "W_df_words": W_df_words,
        "W_df_scales": W_df_scales,
        "W_fc_words": W_fc_words,
        "W_fc_scales": W_fc_scales,
        "b_cf": b_cf,
        "b_df": b_df,
    }


def reference(atom_features, distance_matrix, distance_matrix_mask, W_cf, W_df_words, W_df_scales, W_fc_words, W_fc_scales, b_cf, b_df):
    a = f64(atom_features)
    dist_h = (mxq(f64(distance_matrix), 3, "e4m3") @ unpack_weight(W_df_words, W_df_scales, "e4m3")) + f64(b_df)
    atom_h = a @ f64(W_cf) + f64(b_cf)
    gated = dist_h * atom_h[:, None, :, :]
    out = mxq(gated, 3, "e4m3") @ unpack_weight(W_fc_words, W_fc_scales, "e4m3")
    out = out * f64(distance_matrix_mask)[..., None]
    return np.tanh(out).sum(axis=2) + a

@@ -1,0 +1,301 @@
+from contextlib import ExitStack
+
+import concourse.masks as masks
+import concourse.mybir as mybir
+
+F32 = mybir.dt.float32
+BF16 = mybir.dt.bfloat16
+I32 = mybir.dt.int32
+U32 = mybir.dt.uint32
+U8 = mybir.dt.uint8
+FP8X4 = mybir.dt.float8_e4m3fn_x4
+ADD = mybir.AluOpType.add
+MULT = mybir.AluOpType.mult
+
+P = 128
+PACK = 4
+K_PASS = P * PACK
+MOLS, ATOMS = 16, 8
+NF, ND, NH = 512, 8192, 512
+GROUPS = ND // K_PASS
+ROW_TILES = ATOMS
+PAIR = 2
+PAIRS = ROW_TILES // PAIR
+CHUNK_GROUPS = 4
+CHUNKS = GROUPS // CHUNK_GROUPS
+CHUNK_K = CHUNK_GROUPS * K_PASS
+UNITS = PAIR * CHUNK_GROUPS
+BATCHES = PAIRS * CHUNKS
+BANK_UNITS = 2
+HALF_UNITS = UNITS // 2
+WORDS = K_PASS // 2
+NF_TILES = NF // P
+STEPS_AFTER = 4
+
+FLOPS = 2 * MOLS * ATOMS * ATOMS * ND * NH + 2 * MOLS * ATOMS * NF * NH + 2 * MOLS * ATOMS * ATOMS * NH * NF
+
+
+def tile_due(n, lag):
+    pair, member = divmod(n - lag - CHUNKS, CHUNKS)
+    if 0 <= pair < PAIRS and member < PAIR:
+        return PAIR * pair + member
+    return None
+
+
+def tile_dtnnstep_pa_k_kernel(
+    tc,
+    atom_features,
+    distance_matrix,
+    distance_matrix_mask,
+    W_cf,
+    W_df_words,
+    W_df_scales,
+    W_fc_words,
+    W_fc_scales,
+    b_cf,
+    b_df,
+    out,
+):
+    nc = tc.nc
+    with ExitStack() as stack:
+        keep = stack.enter_context(tc.tile_pool(name="keep", bufs=1))
+        work = stack.enter_context(tc.tile_pool(name="work", bufs=2))
+        sum_banks = stack.enter_context(tc.psum_pool(name="sum_banks", bufs=PAIR))
+        word_banks = stack.enter_context(tc.psum_pool(name="word_banks", bufs=UNITS // BANK_UNITS))
+        flip_bank = stack.enter_context(tc.psum_pool(name="flip_bank", bufs=1))
+        late_bank = stack.enter_context(tc.psum_pool(name="late_bank", bufs=1))
+        stack.enter_context(tc.manual_schedule())
+
+        ident_f32 = keep.tile([P, P], F32, name="ident_f32")
+        masks.make_identity(nc, ident_f32[:])
+        ident_bf16 = keep.tile([P, P], BF16, name="ident_bf16")
+        masks.make_identity(nc, ident_bf16[:])
+
+        df_planes = keep.tile([P, CHUNKS, NH], U8, name="df_planes", align_bytes=64)
+        fc_plane = keep.tile([P, NF], U8, name="fc_plane", align_bytes=64)
+        nc.vector.memset(df_planes[:].bitcast(I32), 0)
+        nc.vector.memset(fc_plane[:].bitcast(I32), 0)
+
+        dist = {}
+        df_words = {}
+
+        def load_distances(i, c):
+            dist[(i, c)] = keep.tile([P, CHUNK_K], BF16, name="dist_%d_%d" % (i, c))
+            nc.sync.dma_start(out=dist[(i, c)][:], in_=distance_matrix[:, i, :, c * CHUNK_K : (c + 1) * CHUNK_K])
+
+        def load_df_words(c):
+            df_words[c] = keep.tile([P, CHUNK_GROUPS, NH], U32, name="df_words_%d" % c, align_bytes=64)
+            groups = W_df_words[c * CHUNK_GROUPS : (c + 1) * CHUNK_GROUPS]
+            nc.sync.dma_start(
+                out=df_words[c][:].bitcast(I32),
+                in_=groups.rearrange("g p n t -> p g (n t)").bitcast(I32),
+            )
+
+        def load_df_scales():
+            for c in range(CHUNKS):
+                for quadrant in range(4):
+                    nc.sync.dma_start(
+                        out=df_planes[32 * quadrant : 32 * quadrant + 16, c, :].bitcast(I32),
+                        in_=W_df_scales[
+                            c * CHUNK_GROUPS : (c + 1) * CHUNK_GROUPS, 4 * quadrant : 4 * quadrant + 4, :
+                        ].bitcast(I32),
+                    )
+
+        for i in range(PAIR):
+            load_distances(i, 0)
+        load_df_scales()
+        load_df_words(0)
+        for c in range(1, CHUNKS):
+            for i in range(PAIR):
+                load_distances(i, c)
+            load_df_words(c)
+
+        bdf_all = keep.tile([P, NH], BF16, name="bdf_all")
+        nc.sync.dma_start(out=bdf_all[:], in_=b_df.partition_broadcast(P))
+        atoms = keep.tile([P, NF], BF16, name="atoms")
+        nc.sync.dma_start(out=atoms[:], in_=atom_features.flatten_outer_dims())
+        cf_rows = keep.tile([P, NF // P, NH], BF16, name="cf_rows")
+        nc.sync.dma_start(out=cf_rows[:], in_=W_cf.rearrange("(c p) n -> p c n", p=P))
+        bcf_all = keep.tile([P, NH], BF16, name="bcf_all")
+        nc.sync.dma_start(out=bcf_all[:], in_=b_cf.partition_broadcast(P))
+        fc_words = keep.tile([P, NF], U32, name="fc_words", align_bytes=64)
+        nc.sync.dma_start(
+            out=fc_words[:].bitcast(I32), in_=W_fc_words[0].rearrange("p n t -> p (n t)").bitcast(I32)
+        )
+        for quadrant in range(4):
+            nc.sync.dma_start(
+                out=fc_plane[32 * quadrant : 32 * quadrant + 4, :].bitcast(I32),
+                in_=W_fc_scales[0, 4 * quadrant : 4 * quadrant + 4, :].bitcast(I32),
+            )
+        weight_all = keep.tile([P, MOLS, ATOMS, ATOMS], BF16, name="weight_all")
+        nc.sync.dma_start(
+            out=weight_all[:].rearrange("p b i j -> p (b i j)"),
+            in_=distance_matrix_mask.rearrange("b i j -> (b i j)").partition_broadcast(P),
+        )
+
+        for pair in range(1, PAIRS):
+            for c in range(CHUNKS):
+                for member in range(PAIR):
+                    load_distances(PAIR * pair + member, c)
+
+        flipped = {}
+        quantised = {}
+        sums = {}
+
+        def unit_of(n, unit):
+            pair, c = divmod(n, CHUNKS)
+            member, g = divmod(unit, CHUNK_GROUPS)
+            return PAIR * pair + member, c, g
+
+        def transpose_batch(n):
+            flipped[n] = []
+            for first in range(0, UNITS, BANK_UNITS):
+                bank = word_banks.tile([P, BANK_UNITS, 2, P], F32, name="bank")
+                for s in range(BANK_UNITS):
+                    i, c, g = unit_of(n, first + s)
+                    words = dist[(i, c)][:].bitcast(F32)
+                    for u in range(2):
+                        nc.tensor.transpose(
+                            bank[:, s, u, :], words[:, g * WORDS + u : (g + 1) * WORDS : 2], ident_f32[:]
+                        )
+                flipped[n].append(bank)
+
+        def quantise_batch(n):
+            grouped = work.tile([P, UNITS, P, PACK], BF16, name="grouped", align_bytes=64)
+            codes = work.tile([P, UNITS, P], U32, name="codes", align_bytes=64)
+            scales = work.tile([P, UNITS, P], U8, name="scales", align_bytes=64)
+            for first in range(0, UNITS, HALF_UNITS):
+                for unit in range(first, first + HALF_UNITS, BANK_UNITS):
+                    nc.scalar.copy(
+                        out=grouped[:, unit : unit + BANK_UNITS].bitcast(F32),
+                        in_=flipped[n][unit // BANK_UNITS][:].rearrange("p s u r -> p s r u"),
+                    )
+                half = slice(first, first + HALF_UNITS)
+                nc.vector.quantize_mx(
+                    out=codes[:, half].rearrange("p s r -> p (s r)").bitcast(FP8X4),
+                    scales=scales[:, half].rearrange("p s r -> p (s r)"),
+                    in_=grouped[:, half].rearrange("p s r t -> p (s r t)"),
+                )
+            quantised[n] = (codes, scales)
+
+        def multiply_batch(n):
+            codes, scales = quantised[n]
+            for unit in range(UNITS):
+                i, c, g = unit_of(n, unit)
+                if c == 0 and g == 0:
+                    sums[i] = sum_banks.tile([P, NH], F32, name="dist_sum")
+                nc.tensor.matmul_mx(
+                    out=sums[i][:],
+                    lhsT=codes[:, unit, :].bitcast(FP8X4),
+                    lhsT_scale=scales[:, unit, :],
+                    rhs=df_words[c][:, g, :].bitcast(FP8X4),
+                    rhs_scale=df_planes[PACK * g : P, c, :],
+                    start=(c == 0 and g == 0),
+                    stop=(c == CHUNKS - 1 and g == CHUNK_GROUPS - 1),
+                )
+
+        atom_h = keep.tile([P, NH], F32, name="atom_h")
+        atoms_t = keep.tile([P, NF // P, P], BF16, name="atoms_t")
+        atoms_flip = {}
+
+        def transpose_atoms():
+            atoms_flip[0] = flip_bank.tile([P, NF // P, P], BF16, name="flip")
+            for c in range(NF // P):
+                nc.tensor.transpose(atoms_flip[0][:, c, :], atoms[:, c * P : (c + 1) * P], ident_bf16[:])
+
+        def atom_hidden():
+            nc.scalar.copy(out=atoms_t[:], in_=atoms_flip[0][:])
+            product = late_bank.tile([P, NH], F32, name="late")
+            for c in range(NF // P):
+                nc.tensor.matmul(
+                    out=product[:], lhsT=atoms_t[:, c, :], rhs=cf_rows[:, c, :], start=(c == 0), stop=(c == NF // P - 1)
+                )
+            nc.vector.tensor_tensor(out=atom_h[:], in0=product[:], in1=bcf_all[:], op=ADD)
+
+        biased = {}
+        gated = {}
+        gated_flip = {}
+        gated_mx = {}
+        products = {}
+        sums_t = keep.tile([P, NF_TILES, MOLS, ATOMS], F32, name="sums_t")
+
+        def add_bias(i):
+            biased[i] = work.tile([P, NH], F32, name="biased")
+            nc.vector.tensor_tensor(out=biased[i][:], in0=sums[i][:], in1=bdf_all[:], op=ADD)
+
+        def gate(i):
+            gated[i] = work.tile([P, NH], BF16, name="gated")
+            nc.vector.tensor_tensor(out=gated[i][:], in0=biased[i][:], in1=atom_h[:], op=MULT)
+
+        def transpose_gated(i):
+            gated_flip[i] = flip_bank.tile([P, PACK, P], BF16, name="flip")
+            for t in range(PACK):
+                nc.tensor.transpose(gated_flip[i][:, t, :], gated[i][:, t:NH:PACK], ident_bf16[:])
+
+        def quantise_gated(i):
+            grouped = work.tile([P, P, PACK], BF16, name="gated_grouped", align_bytes=64)
+            codes = work.tile([P, P], U32, name="gated_codes", align_bytes=64)
+            scales = work.tile([P, P], U8, name="gated_scales", align_bytes=64)
+            nc.scalar.copy(out=grouped[:], in_=gated_flip[i][:].rearrange("p t r -> p r t"))
+            nc.vector.quantize_mx(
+                out=codes[:].bitcast(FP8X4), scales=scales[:], in_=grouped[:].rearrange("p r t -> p (r t)")
+            )
+            gated_mx[i] = (codes, scales)
+
+        def multiply_gated(i):
+            codes, scales = gated_mx[i]
+            products[i] = late_bank.tile([P, NF_TILES, P], F32, name="late")
+            for m in range(NF_TILES):
+                nc.tensor.matmul_mx(
+                    out=products[i][:, m, :],
+                    lhsT=fc_words[:, m * P : (m + 1) * P].bitcast(FP8X4),
+                    lhsT_scale=fc_plane[:, m * P : (m + 1) * P],
+                    rhs=codes[:].bitcast(FP8X4),
+                    rhs_scale=scales[:],
+                    start=True,
+                    stop=True,
+                )
+
+        def sum_over_j(i):
+            weighted = work.tile([P, NF_TILES, MOLS, ATOMS], F32, name="weighted")
+            nc.vector.tensor_tensor(
+                out=weighted[:],
+                in0=products[i][:].rearrange("p m (b j) -> p m b j", j=ATOMS),
+                in1=weight_all[:, :, i, :].unsqueeze(1).to_broadcast([P, NF_TILES, MOLS, ATOMS]),
+                op=MULT,
+            )
+            nc.scalar.activation(out=weighted[:], in_=weighted[:], func=mybir.ActivationFunctionType.Tanh)
+            nc.vector.tensor_reduce(out=sums_t[:, :, :, i], in_=weighted[:], axis=mybir.AxisListType.X, op=ADD)
+
+        for n in range(BATCHES + STEPS_AFTER):
+            to_gate, to_flip, to_finish = tile_due(n, 0), tile_due(n, 1), tile_due(n, 2)
+            if n < BATCHES:
+                transpose_batch(n)
+            if n == CHUNKS:
+                transpose_atoms()
+            if to_flip is not None:
+                transpose_gated(to_flip)
+            if 1 <= n <= BATCHES:
+                multiply_batch(n - 1)
+            if to_finish is not None:
+                multiply_gated(to_finish)
+            if n < BATCHES:
+                quantise_batch(n)
+            if 1 <= n <= BATCHES and n % CHUNKS == 0:
+                for member in range(PAIR):
+                    add_bias(n // CHUNKS * PAIR - PAIR + member)
+            if n == CHUNKS:
+                atom_hidden()
+            if to_gate is not None:
+                gate(to_gate)
+            if to_flip is not None:
+                quantise_gated(to_flip)
+            if to_finish is not None:
+                sum_over_j(to_finish)
+
+        final = late_bank.tile([P, NF_TILES, P], F32, name="late")
+        for m in range(NF_TILES):
+            nc.tensor.transpose(final[:, m, :], sums_t[:, m].rearrange("p b i -> p (b i)"), ident_f32[:])
+        result = keep.tile([P, NF], F32, name="result")
+        nc.vector.tensor_tensor(out=result[:], in0=final[:].rearrange("p m f -> p (m f)"), in1=atoms[:], op=ADD)
+        nc.sync.dma_start(out=out.flatten_outer_dims(), in_=result[:])

@@ -24,21 +24,27 @@ PAIRS = ROW_TILES // PAIR
 CHUNK_GROUPS = 4
 CHUNKS = GROUPS // CHUNK_GROUPS
 CHUNK_K = CHUNK_GROUPS * K_PASS
-UNITS = PAIR * CHUNK_GROUPS
-BATCHES = PAIRS * CHUNKS
+UNITS = CHUNK_GROUPS
+BATCHES = ROW_TILES * CHUNKS
 BANK_UNITS = 2
-HALF_UNITS = UNITS // 2
+LAG = 2
 WORDS = K_PASS // 2
 NF_TILES = NF // P
-STEPS_AFTER = 4
+LATE_STEPS = 2
 
 FLOPS = 2 * MOLS * ATOMS * ATOMS * ND * NH + 2 * MOLS * ATOMS * NF * NH + 2 * MOLS * ATOMS * ATOMS * NH * NF
 
 
-def tile_due(n, lag):
-    pair, member = divmod(n - lag - CHUNKS, CHUNKS)
-    if 0 <= pair < PAIRS and member < PAIR:
-        return PAIR * pair + member
+def batch_of(n):
+    pair, rest = divmod(n, PAIR * CHUNKS)
+    c, member = divmod(rest, PAIR)
+    return PAIR * pair + member, c
+
+
+def tile_due(n, step):
+    batch = n - step - LAG
+    if 0 <= batch < BATCHES and batch_of(batch)[1] == CHUNKS - 1:
+        return batch_of(batch)[0]
     return None
 
 
@@ -60,8 +66,9 @@ def tile_dtnnstep_pa_k_kernel(
     with ExitStack() as stack:
         keep = stack.enter_context(tc.tile_pool(name="keep", bufs=1))
         work = stack.enter_context(tc.tile_pool(name="work", bufs=2))
+        operands = stack.enter_context(tc.tile_pool(name="operands", bufs=LAG + 2))
         sum_banks = stack.enter_context(tc.psum_pool(name="sum_banks", bufs=PAIR))
-        word_banks = stack.enter_context(tc.psum_pool(name="word_banks", bufs=UNITS // BANK_UNITS))
+        word_banks = stack.enter_context(tc.psum_pool(name="word_banks", bufs=2 * UNITS // BANK_UNITS))
         flip_bank = stack.enter_context(tc.psum_pool(name="flip_bank", bufs=1))
         late_bank = stack.enter_context(tc.psum_pool(name="late_bank", bufs=1))
         stack.enter_context(tc.manual_schedule())
@@ -142,18 +149,13 @@ def tile_dtnnstep_pa_k_kernel(
         quantised = {}
         sums = {}
 
-        def unit_of(n, unit):
-            pair, c = divmod(n, CHUNKS)
-            member, g = divmod(unit, CHUNK_GROUPS)
-            return PAIR * pair + member, c, g
-
         def transpose_batch(n):
+            words = dist[batch_of(n)][:].bitcast(F32)
             flipped[n] = []
             for first in range(0, UNITS, BANK_UNITS):
                 bank = word_banks.tile([P, BANK_UNITS, 2, P], F32, name="bank")
                 for s in range(BANK_UNITS):
-                    i, c, g = unit_of(n, first + s)
-                    words = dist[(i, c)][:].bitcast(F32)
+                    g = first + s
                     for u in range(2):
                         nc.tensor.transpose(
                             bank[:, s, u, :], words[:, g * WORDS + u : (g + 1) * WORDS : 2], ident_f32[:]
@@ -162,32 +164,30 @@ def tile_dtnnstep_pa_k_kernel(
 
         def quantise_batch(n):
             grouped = work.tile([P, UNITS, P, PACK], BF16, name="grouped", align_bytes=64)
-            codes = work.tile([P, UNITS, P], U32, name="codes", align_bytes=64)
-            scales = work.tile([P, UNITS, P], U8, name="scales", align_bytes=64)
-            for first in range(0, UNITS, HALF_UNITS):
-                for unit in range(first, first + HALF_UNITS, BANK_UNITS):
-                    nc.scalar.copy(
-                        out=grouped[:, unit : unit + BANK_UNITS].bitcast(F32),
-                        in_=flipped[n][unit // BANK_UNITS][:].rearrange("p s u r -> p s r u"),
-                    )
-                half = slice(first, first + HALF_UNITS)
-                nc.vector.quantize_mx(
-                    out=codes[:, half].rearrange("p s r -> p (s r)").bitcast(FP8X4),
-                    scales=scales[:, half].rearrange("p s r -> p (s r)"),
-                    in_=grouped[:, half].rearrange("p s r t -> p (s r t)"),
+            codes = operands.tile([P, UNITS, P], U32, name="codes", align_bytes=64)
+            scales = operands.tile([P, UNITS, P], U8, name="scales", align_bytes=64)
+            for first in range(0, UNITS, BANK_UNITS):
+                nc.scalar.copy(
+                    out=grouped[:, first : first + BANK_UNITS].bitcast(F32),
+                    in_=flipped[n][first // BANK_UNITS][:].rearrange("p s u r -> p s r u"),
                 )
+            nc.vector.quantize_mx(
+                out=codes[:].rearrange("p s r -> p (s r)").bitcast(FP8X4),
+                scales=scales[:].rearrange("p s r -> p (s r)"),
+                in_=grouped[:].rearrange("p s r t -> p (s r t)"),
+            )
             quantised[n] = (codes, scales)
 
         def multiply_batch(n):
+            i, c = batch_of(n)
             codes, scales = quantised[n]
-            for unit in range(UNITS):
-                i, c, g = unit_of(n, unit)
-                if c == 0 and g == 0:
-                    sums[i] = sum_banks.tile([P, NH], F32, name="dist_sum")
+            if c == 0:
+                sums[i] = sum_banks.tile([P, NH], F32, name="dist_sum")
+            for g in range(UNITS):
                 nc.tensor.matmul_mx(
                     out=sums[i][:],
-                    lhsT=codes[:, unit, :].bitcast(FP8X4),
-                    lhsT_scale=scales[:, unit, :],
+                    lhsT=codes[:, g, :].bitcast(FP8X4),
+                    lhsT_scale=scales[:, g, :],
                     rhs=df_words[c][:, g, :].bitcast(FP8X4),
                     rhs_scale=df_planes[PACK * g : P, c, :],
                     start=(c == 0 and g == 0),
@@ -267,24 +267,24 @@ def tile_dtnnstep_pa_k_kernel(
             nc.scalar.activation(out=weighted[:], in_=weighted[:], func=mybir.ActivationFunctionType.Tanh)
             nc.vector.tensor_reduce(out=sums_t[:, :, :, i], in_=weighted[:], axis=mybir.AxisListType.X, op=ADD)
 
-        for n in range(BATCHES + STEPS_AFTER):
+        atom_round = PAIR * (CHUNKS - 1) + LAG
+        for n in range(BATCHES + LAG + LATE_STEPS):
             to_gate, to_flip, to_finish = tile_due(n, 0), tile_due(n, 1), tile_due(n, 2)
             if n < BATCHES:
                 transpose_batch(n)
-            if n == CHUNKS:
+            if n == atom_round:
                 transpose_atoms()
             if to_flip is not None:
                 transpose_gated(to_flip)
-            if 1 <= n <= BATCHES:
-                multiply_batch(n - 1)
+            if 0 <= n - LAG < BATCHES:
+                multiply_batch(n - LAG)
             if to_finish is not None:
                 multiply_gated(to_finish)
             if n < BATCHES:
                 quantise_batch(n)
-            if 1 <= n <= BATCHES and n % CHUNKS == 0:
-                for member in range(PAIR):
-                    add_bias(n // CHUNKS * PAIR - PAIR + member)
-            if n == CHUNKS:
+            if to_gate is not None:
+                add_bias(to_gate)
+            if n == atom_round:
                 atom_hidden()
             if to_gate is not None:
                 gate(to_gate)

@@ -15,37 +15,31 @@ MULT = mybir.AluOpType.mult
 P = 128
 PACK = 4
 K_PASS = P * PACK
+BANK = 512
 MOLS, ATOMS = 16, 8
 NF, ND, NH = 512, 8192, 512
 GROUPS = ND // K_PASS
 ROW_TILES = ATOMS
 PAIR = 2
-PAIRS = ROW_TILES // PAIR
 CHUNK_GROUPS = 4
 CHUNKS = GROUPS // CHUNK_GROUPS
 CHUNK_K = CHUNK_GROUPS * K_PASS
-UNITS = CHUNK_GROUPS
 BATCHES = ROW_TILES * CHUNKS
-BANK_UNITS = 2
-LAG = 2
+BANK_GROUPS = 2
+RUN = 2
+LAG = 1
+ROUNDS = BATCHES // RUN
 WORDS = K_PASS // 2
 NF_TILES = NF // P
-LATE_STEPS = 2
+PAIRS_OF_ATOMS = MOLS * ATOMS * ATOMS
 
-FLOPS = 2 * MOLS * ATOMS * ATOMS * ND * NH + 2 * MOLS * ATOMS * NF * NH + 2 * MOLS * ATOMS * ATOMS * NH * NF
+FLOPS = 2 * PAIRS_OF_ATOMS * ND * NH + 2 * MOLS * ATOMS * NF * NH + 2 * PAIRS_OF_ATOMS * NH * NF
 
 
 def batch_of(n):
     pair, rest = divmod(n, PAIR * CHUNKS)
     c, member = divmod(rest, PAIR)
     return PAIR * pair + member, c
-
-
-def tile_due(n, step):
-    batch = n - step - LAG
-    if 0 <= batch < BATCHES and batch_of(batch)[1] == CHUNKS - 1:
-        return batch_of(batch)[0]
-    return None
 
 
 def tile_dtnnstep_pa_k_kernel(
@@ -66,19 +60,23 @@ def tile_dtnnstep_pa_k_kernel(
     with ExitStack() as stack:
         keep = stack.enter_context(tc.tile_pool(name="keep", bufs=1))
         work = stack.enter_context(tc.tile_pool(name="work", bufs=2))
-        operands = stack.enter_context(tc.tile_pool(name="operands", bufs=LAG + 2))
+        operands = stack.enter_context(tc.tile_pool(name="operands", bufs=RUN * (LAG + 1)))
         sum_banks = stack.enter_context(tc.psum_pool(name="sum_banks", bufs=PAIR))
-        word_banks = stack.enter_context(tc.psum_pool(name="word_banks", bufs=2 * UNITS // BANK_UNITS))
+        word_banks = stack.enter_context(tc.psum_pool(name="word_banks", bufs=RUN * CHUNK_GROUPS // BANK_GROUPS))
         flip_bank = stack.enter_context(tc.psum_pool(name="flip_bank", bufs=1))
         late_bank = stack.enter_context(tc.psum_pool(name="late_bank", bufs=1))
         stack.enter_context(tc.manual_schedule())
 
+        rows = keep.tile([P, 2 * NH + PAIRS_OF_ATOMS], BF16, name="rows")
+        nc.vector.memset(rows[:].bitcast(I32), 0)
+        ones = keep.tile([P, P], BF16, name="ones")
+        nc.vector.memset(ones[:], 1.0)
         ident_f32 = keep.tile([P, P], F32, name="ident_f32")
         masks.make_identity(nc, ident_f32[:])
         ident_bf16 = keep.tile([P, P], BF16, name="ident_bf16")
         masks.make_identity(nc, ident_bf16[:])
 
-        df_planes = keep.tile([P, CHUNKS, NH], U8, name="df_planes", align_bytes=64)
+        df_planes = keep.tile([P, GROUPS, NH], U8, name="df_planes", align_bytes=64)
         fc_plane = keep.tile([P, NF], U8, name="fc_plane", align_bytes=64)
         nc.vector.memset(df_planes[:].bitcast(I32), 0)
         nc.vector.memset(fc_plane[:].bitcast(I32), 0)
@@ -98,53 +96,48 @@ def tile_dtnnstep_pa_k_kernel(
                 in_=groups.rearrange("g p n t -> p g (n t)").bitcast(I32),
             )
 
-        def load_df_scales():
-            for c in range(CHUNKS):
-                for quadrant in range(4):
-                    nc.sync.dma_start(
-                        out=df_planes[32 * quadrant : 32 * quadrant + 16, c, :].bitcast(I32),
-                        in_=W_df_scales[
-                            c * CHUNK_GROUPS : (c + 1) * CHUNK_GROUPS, 4 * quadrant : 4 * quadrant + 4, :
-                        ].bitcast(I32),
-                    )
-
-        for i in range(PAIR):
-            load_distances(i, 0)
-        load_df_scales()
-        load_df_words(0)
-        for c in range(1, CHUNKS):
+        nc.sync.dma_start(out=rows[0:1, 0:NH], in_=b_df.unsqueeze(0))
+        nc.sync.dma_start(out=rows[0:1, NH : 2 * NH], in_=b_cf.unsqueeze(0))
+        nc.sync.dma_start(
+            out=rows[0:1, 2 * NH :], in_=distance_matrix_mask.rearrange("b i j -> (b i j)").unsqueeze(0)
+        )
+        for c in range(CHUNKS):
             for i in range(PAIR):
                 load_distances(i, c)
+            if c == 0:
+                for r in range(4):
+                    nc.sync.dma_start(
+                        out=df_planes[r:P:32, :, :].bitcast(I32),
+                        in_=W_df_scales[:, r:16:4, :].rearrange("g q n -> q g n").bitcast(I32),
+                    )
             load_df_words(c)
-
-        bdf_all = keep.tile([P, NH], BF16, name="bdf_all")
-        nc.sync.dma_start(out=bdf_all[:], in_=b_df.partition_broadcast(P))
+        for n in range(PAIR * CHUNKS, PAIR * CHUNKS + RUN):
+            load_distances(*batch_of(n))
         atoms = keep.tile([P, NF], BF16, name="atoms")
         nc.sync.dma_start(out=atoms[:], in_=atom_features.flatten_outer_dims())
         cf_rows = keep.tile([P, NF // P, NH], BF16, name="cf_rows")
         nc.sync.dma_start(out=cf_rows[:], in_=W_cf.rearrange("(c p) n -> p c n", p=P))
-        bcf_all = keep.tile([P, NH], BF16, name="bcf_all")
-        nc.sync.dma_start(out=bcf_all[:], in_=b_cf.partition_broadcast(P))
         fc_words = keep.tile([P, NF], U32, name="fc_words", align_bytes=64)
         nc.sync.dma_start(
             out=fc_words[:].bitcast(I32), in_=W_fc_words[0].rearrange("p n t -> p (n t)").bitcast(I32)
         )
-        for quadrant in range(4):
-            nc.sync.dma_start(
-                out=fc_plane[32 * quadrant : 32 * quadrant + 4, :].bitcast(I32),
-                in_=W_fc_scales[0, 4 * quadrant : 4 * quadrant + 4, :].bitcast(I32),
-            )
+        for r in range(4):
+            nc.sync.dma_start(out=fc_plane[r:P:32, :].bitcast(I32), in_=W_fc_scales[0, r:16:4, :].bitcast(I32))
+        for n in range(PAIR * CHUNKS + RUN, BATCHES):
+            load_distances(*batch_of(n))
+
+        bdf_all = keep.tile([P, NH], BF16, name="bdf_all")
         weight_all = keep.tile([P, MOLS, ATOMS, ATOMS], BF16, name="weight_all")
-        nc.sync.dma_start(
-            out=weight_all[:].rearrange("p b i j -> p (b i j)"),
-            in_=distance_matrix_mask.rearrange("b i j -> (b i j)").partition_broadcast(P),
-        )
+        weight_flat = weight_all[:].rearrange("p b i j -> p (b i j)")
 
-        for pair in range(1, PAIRS):
-            for c in range(CHUNKS):
-                for member in range(PAIR):
-                    load_distances(PAIR * pair + member, c)
+        def spread(columns, target):
+            bank = word_banks.tile([P, BANK], F32, name="bank")
+            nc.tensor.matmul(out=bank[:], lhsT=ones[:], rhs=rows[:, columns], start=True, stop=True)
+            nc.vector.tensor_copy(out=target, in_=bank[:])
 
+        spread(slice(0, NH), bdf_all[:])
+        for first in range(0, PAIRS_OF_ATOMS, BANK):
+            spread(slice(2 * NH + first, 2 * NH + first + BANK), weight_flat[:, first : first + BANK])
         flipped = {}
         quantised = {}
         sums = {}
@@ -152,9 +145,9 @@ def tile_dtnnstep_pa_k_kernel(
         def transpose_batch(n):
             words = dist[batch_of(n)][:].bitcast(F32)
             flipped[n] = []
-            for first in range(0, UNITS, BANK_UNITS):
-                bank = word_banks.tile([P, BANK_UNITS, 2, P], F32, name="bank")
-                for s in range(BANK_UNITS):
+            for first in range(0, CHUNK_GROUPS, BANK_GROUPS):
+                bank = word_banks.tile([P, BANK_GROUPS, 2, P], F32, name="bank")
+                for s in range(BANK_GROUPS):
                     g = first + s
                     for u in range(2):
                         nc.tensor.transpose(
@@ -163,13 +156,13 @@ def tile_dtnnstep_pa_k_kernel(
                 flipped[n].append(bank)
 
         def quantise_batch(n):
-            grouped = work.tile([P, UNITS, P, PACK], BF16, name="grouped", align_bytes=64)
-            codes = operands.tile([P, UNITS, P], U32, name="codes", align_bytes=64)
-            scales = operands.tile([P, UNITS, P], U8, name="scales", align_bytes=64)
-            for first in range(0, UNITS, BANK_UNITS):
+            grouped = work.tile([P, CHUNK_GROUPS, P, PACK], BF16, name="grouped", align_bytes=64)
+            codes = operands.tile([P, CHUNK_GROUPS, P], U32, name="codes", align_bytes=64)
+            scales = operands.tile([P, CHUNK_GROUPS, P], U8, name="scales", align_bytes=64)
+            for first in range(0, CHUNK_GROUPS, BANK_GROUPS):
                 nc.scalar.copy(
-                    out=grouped[:, first : first + BANK_UNITS].bitcast(F32),
-                    in_=flipped[n][first // BANK_UNITS][:].rearrange("p s u r -> p s r u"),
+                    out=grouped[:, first : first + BANK_GROUPS].bitcast(F32),
+                    in_=flipped[n][first // BANK_GROUPS][:].rearrange("p s u r -> p s r u"),
                 )
             nc.vector.quantize_mx(
                 out=codes[:].rearrange("p s r -> p (s r)").bitcast(FP8X4),
@@ -183,13 +176,13 @@ def tile_dtnnstep_pa_k_kernel(
             codes, scales = quantised[n]
             if c == 0:
                 sums[i] = sum_banks.tile([P, NH], F32, name="dist_sum")
-            for g in range(UNITS):
+            for g in range(CHUNK_GROUPS):
                 nc.tensor.matmul_mx(
                     out=sums[i][:],
                     lhsT=codes[:, g, :].bitcast(FP8X4),
                     lhsT_scale=scales[:, g, :],
                     rhs=df_words[c][:, g, :].bitcast(FP8X4),
-                    rhs_scale=df_planes[PACK * g : P, c, :],
+                    rhs_scale=df_planes[:, c * CHUNK_GROUPS + g, :],
                     start=(c == 0 and g == 0),
                     stop=(c == CHUNKS - 1 and g == CHUNK_GROUPS - 1),
                 )
@@ -207,10 +200,9 @@ def tile_dtnnstep_pa_k_kernel(
             nc.scalar.copy(out=atoms_t[:], in_=atoms_flip[0][:])
             product = late_bank.tile([P, NH], F32, name="late")
             for c in range(NF // P):
-                nc.tensor.matmul(
-                    out=product[:], lhsT=atoms_t[:, c, :], rhs=cf_rows[:, c, :], start=(c == 0), stop=(c == NF // P - 1)
-                )
-            nc.vector.tensor_tensor(out=atom_h[:], in0=product[:], in1=bcf_all[:], op=ADD)
+                nc.tensor.matmul(out=product[:], lhsT=atoms_t[:, c, :], rhs=cf_rows[:, c, :], start=(c == 0), stop=False)
+            nc.tensor.matmul(out=product[:], lhsT=ones[:], rhs=rows[:, NH : 2 * NH], start=False, stop=True)
+            nc.vector.tensor_copy(out=atom_h[:], in_=product[:])
 
         biased = {}
         gated = {}
@@ -267,26 +259,37 @@ def tile_dtnnstep_pa_k_kernel(
             nc.scalar.activation(out=weighted[:], in_=weighted[:], func=mybir.ActivationFunctionType.Tanh)
             nc.vector.tensor_reduce(out=sums_t[:, :, :, i], in_=weighted[:], axis=mybir.AxisListType.X, op=ADD)
 
-        atom_round = PAIR * (CHUNKS - 1) + LAG
-        for n in range(BATCHES + LAG + LATE_STEPS):
-            to_gate, to_flip, to_finish = tile_due(n, 0), tile_due(n, 1), tile_due(n, 2)
-            if n < BATCHES:
-                transpose_batch(n)
+        first_end = PAIR * CHUNKS // RUN - 1 + LAG
+        atom_round = first_end + 1
+        finished = []
+        entered = 0
+        to_gate, to_flip = None, None
+        for n in range(ROUNDS + LAG + PAIR - 1 + 2):
+            to_finish, to_flip = to_flip, to_gate
+            fresh = range(RUN * n, RUN * n + RUN) if n < ROUNDS else ()
+            ripe = range(RUN * (n - LAG), RUN * (n - LAG) + RUN) if 0 <= n - LAG < ROUNDS else ()
+            for batch in fresh:
+                transpose_batch(batch)
             if n == atom_round:
                 transpose_atoms()
             if to_flip is not None:
                 transpose_gated(to_flip)
-            if 0 <= n - LAG < BATCHES:
-                multiply_batch(n - LAG)
+            for batch in ripe:
+                multiply_batch(batch)
             if to_finish is not None:
                 multiply_gated(to_finish)
-            if n < BATCHES:
-                quantise_batch(n)
-            if to_gate is not None:
-                add_bias(to_gate)
+            for batch in fresh:
+                quantise_batch(batch)
+            for batch in ripe:
+                if batch_of(batch)[1] == CHUNKS - 1:
+                    add_bias(batch_of(batch)[0])
+                    finished.append(batch_of(batch)[0])
             if n == atom_round:
                 atom_hidden()
-            if to_gate is not None:
+            to_gate = None
+            if n >= atom_round and entered < len(finished):
+                to_gate = finished[entered]
+                entered += 1
                 gate(to_gate)
             if to_flip is not None:
                 quantise_gated(to_flip)

@@ -29,7 +29,9 @@ BANK_GROUPS = 2
 RUN = 2
 LAG = 1
 ROUNDS = BATCHES // RUN
-WORDS = K_PASS // 2
+assert RUN == PAIR
+LATE_STEPS = 5
+SPREAD_FROM = 2
 NF_TILES = NF // P
 PAIRS_OF_ATOMS = MOLS * ATOMS * ATOMS
 
@@ -37,9 +39,17 @@ FLOPS = 2 * PAIRS_OF_ATOMS * ND * NH + 2 * MOLS * ATOMS * NF * NH + 2 * PAIRS_OF
 
 
 def batch_of(n):
-    pair, rest = divmod(n, PAIR * CHUNKS)
-    c, member = divmod(rest, PAIR)
-    return PAIR * pair + member, c
+    if n < PAIR * CHUNKS:
+        c, i = divmod(n, PAIR)
+    else:
+        i, c = divmod(n, CHUNKS)
+    return i, c
+
+
+def batches_of_round(n):
+    if 0 <= n < ROUNDS:
+        return range(RUN * n, RUN * n + RUN)
+    return range(0)
 
 
 def tile_dtnnstep_pa_k_kernel(
@@ -61,6 +71,7 @@ def tile_dtnnstep_pa_k_kernel(
         keep = stack.enter_context(tc.tile_pool(name="keep", bufs=1))
         work = stack.enter_context(tc.tile_pool(name="work", bufs=2))
         operands = stack.enter_context(tc.tile_pool(name="operands", bufs=RUN * (LAG + 1)))
+        sorted_pool = stack.enter_context(tc.tile_pool(name="sorted_pool", bufs=RUN * 2))
         sum_banks = stack.enter_context(tc.psum_pool(name="sum_banks", bufs=PAIR))
         word_banks = stack.enter_context(tc.psum_pool(name="word_banks", bufs=RUN * CHUNK_GROUPS // BANK_GROUPS))
         flip_bank = stack.enter_context(tc.psum_pool(name="flip_bank", bufs=1))
@@ -76,7 +87,7 @@ def tile_dtnnstep_pa_k_kernel(
         ident_bf16 = keep.tile([P, P], BF16, name="ident_bf16")
         masks.make_identity(nc, ident_bf16[:])
 
-        df_planes = keep.tile([P, GROUPS, NH], U8, name="df_planes", align_bytes=64)
+        df_planes = keep.tile([P, CHUNKS, NH], U8, name="df_planes", align_bytes=64)
         fc_plane = keep.tile([P, NF], U8, name="fc_plane", align_bytes=64)
         nc.vector.memset(df_planes[:].bitcast(I32), 0)
         nc.vector.memset(fc_plane[:].bitcast(I32), 0)
@@ -96,23 +107,30 @@ def tile_dtnnstep_pa_k_kernel(
                 in_=groups.rearrange("g p n t -> p g (n t)").bitcast(I32),
             )
 
-        nc.sync.dma_start(out=rows[0:1, 0:NH], in_=b_df.unsqueeze(0))
-        nc.sync.dma_start(out=rows[0:1, NH : 2 * NH], in_=b_cf.unsqueeze(0))
-        nc.sync.dma_start(
-            out=rows[0:1, 2 * NH :], in_=distance_matrix_mask.rearrange("b i j -> (b i j)").unsqueeze(0)
-        )
+        def load_round(n):
+            for batch in batches_of_round(n):
+                load_distances(*batch_of(batch))
+
+        load_round(0)
         for c in range(CHUNKS):
-            for i in range(PAIR):
-                load_distances(i, c)
+            load_round(c + 1)
             if c == 0:
-                for r in range(4):
-                    nc.sync.dma_start(
-                        out=df_planes[r:P:32, :, :].bitcast(I32),
-                        in_=W_df_scales[:, r:16:4, :].rearrange("g q n -> q g n").bitcast(I32),
-                    )
+                for chunk in range(CHUNKS):
+                    for quadrant in range(4):
+                        nc.sync.dma_start(
+                            out=df_planes[32 * quadrant : 32 * quadrant + 16, chunk, :].bitcast(I32),
+                            in_=W_df_scales[
+                                chunk * CHUNK_GROUPS : (chunk + 1) * CHUNK_GROUPS, 4 * quadrant : 4 * quadrant + 4, :
+                            ].bitcast(I32),
+                        )
             load_df_words(c)
-        for n in range(PAIR * CHUNKS, PAIR * CHUNKS + RUN):
-            load_distances(*batch_of(n))
+            if c == 0:
+                nc.sync.dma_start(out=rows[0:1, 0:NH], in_=b_df.unsqueeze(0))
+                nc.sync.dma_start(out=rows[0:1, NH : 2 * NH], in_=b_cf.unsqueeze(0))
+                nc.sync.dma_start(
+                    out=rows[0:1, 2 * NH :], in_=distance_matrix_mask.rearrange("b i j -> (b i j)").unsqueeze(0)
+                )
+        load_round(CHUNKS + 1)
         atoms = keep.tile([P, NF], BF16, name="atoms")
         nc.sync.dma_start(out=atoms[:], in_=atom_features.flatten_outer_dims())
         cf_rows = keep.tile([P, NF // P, NH], BF16, name="cf_rows")
@@ -123,36 +141,41 @@ def tile_dtnnstep_pa_k_kernel(
         )
         for r in range(4):
             nc.sync.dma_start(out=fc_plane[r:P:32, :].bitcast(I32), in_=W_fc_scales[0, r:16:4, :].bitcast(I32))
-        for n in range(PAIR * CHUNKS + RUN, BATCHES):
-            load_distances(*batch_of(n))
+        for n in range(CHUNKS + 2, ROUNDS):
+            load_round(n)
 
         bdf_all = keep.tile([P, NH], BF16, name="bdf_all")
         weight_all = keep.tile([P, MOLS, ATOMS, ATOMS], BF16, name="weight_all")
         weight_flat = weight_all[:].rearrange("p b i j -> p (b i j)")
 
         def spread(columns, target):
-            bank = word_banks.tile([P, BANK], F32, name="bank")
+            bank = late_bank.tile([P, BANK], F32, name="late")
             nc.tensor.matmul(out=bank[:], lhsT=ones[:], rhs=rows[:, columns], start=True, stop=True)
             nc.vector.tensor_copy(out=target, in_=bank[:])
 
-        spread(slice(0, NH), bdf_all[:])
+        to_spread = [(slice(0, NH), bdf_all[:])]
         for first in range(0, PAIRS_OF_ATOMS, BANK):
-            spread(slice(2 * NH + first, 2 * NH + first + BANK), weight_flat[:, first : first + BANK])
+            to_spread.append((slice(2 * NH + first, 2 * NH + first + BANK), weight_flat[:, first : first + BANK]))
+
+        sorted_words = {}
         flipped = {}
         quantised = {}
         sums = {}
 
+        def sort_batch(n):
+            sorted_words[n] = sorted_pool.tile([P, CHUNK_GROUPS, 2, P], F32, name="sorted_words")
+            nc.vector.tensor_copy(
+                out=sorted_words[n][:],
+                in_=dist[batch_of(n)][:].bitcast(F32).rearrange("p (g w u) -> p g u w", g=CHUNK_GROUPS, u=2),
+            )
+
         def transpose_batch(n):
-            words = dist[batch_of(n)][:].bitcast(F32)
             flipped[n] = []
             for first in range(0, CHUNK_GROUPS, BANK_GROUPS):
                 bank = word_banks.tile([P, BANK_GROUPS, 2, P], F32, name="bank")
                 for s in range(BANK_GROUPS):
-                    g = first + s
                     for u in range(2):
-                        nc.tensor.transpose(
-                            bank[:, s, u, :], words[:, g * WORDS + u : (g + 1) * WORDS : 2], ident_f32[:]
-                        )
+                        nc.tensor.transpose(bank[:, s, u, :], sorted_words[n][:, first + s, u, :], ident_f32[:])
                 flipped[n].append(bank)
 
         def quantise_batch(n):
@@ -182,7 +205,7 @@ def tile_dtnnstep_pa_k_kernel(
                     lhsT=codes[:, g, :].bitcast(FP8X4),
                     lhsT_scale=scales[:, g, :],
                     rhs=df_words[c][:, g, :].bitcast(FP8X4),
-                    rhs_scale=df_planes[:, c * CHUNK_GROUPS + g, :],
+                    rhs_scale=df_planes[PACK * g : P, c, :],
                     start=(c == 0 and g == 0),
                     stop=(c == CHUNKS - 1 and g == CHUNK_GROUPS - 1),
                 )
@@ -207,8 +230,10 @@ def tile_dtnnstep_pa_k_kernel(
         biased = {}
         gated = {}
         gated_flip = {}
+        gated_grouped = {}
         gated_mx = {}
         products = {}
+        weighted = {}
         sums_t = keep.tile([P, NF_TILES, MOLS, ATOMS], F32, name="sums_t")
 
         def add_bias(i):
@@ -224,13 +249,15 @@ def tile_dtnnstep_pa_k_kernel(
             for t in range(PACK):
                 nc.tensor.transpose(gated_flip[i][:, t, :], gated[i][:, t:NH:PACK], ident_bf16[:])
 
+        def regroup_gated(i):
+            gated_grouped[i] = work.tile([P, P, PACK], BF16, name="gated_grouped", align_bytes=64)
+            nc.scalar.copy(out=gated_grouped[i][:], in_=gated_flip[i][:].rearrange("p t r -> p r t"))
+
         def quantise_gated(i):
-            grouped = work.tile([P, P, PACK], BF16, name="gated_grouped", align_bytes=64)
             codes = work.tile([P, P], U32, name="gated_codes", align_bytes=64)
             scales = work.tile([P, P], U8, name="gated_scales", align_bytes=64)
-            nc.scalar.copy(out=grouped[:], in_=gated_flip[i][:].rearrange("p t r -> p r t"))
             nc.vector.quantize_mx(
-                out=codes[:].bitcast(FP8X4), scales=scales[:], in_=grouped[:].rearrange("p r t -> p (r t)")
+                out=codes[:].bitcast(FP8X4), scales=scales[:], in_=gated_grouped[i][:].rearrange("p r t -> p (r t)")
             )
             gated_mx[i] = (codes, scales)
 
@@ -248,53 +275,69 @@ def tile_dtnnstep_pa_k_kernel(
                     stop=True,
                 )
 
-        def sum_over_j(i):
-            weighted = work.tile([P, NF_TILES, MOLS, ATOMS], F32, name="weighted")
+        def weigh(i):
+            weighted[i] = work.tile([P, NF_TILES, MOLS, ATOMS], F32, name="weighted")
             nc.vector.tensor_tensor(
-                out=weighted[:],
+                out=weighted[i][:],
                 in0=products[i][:].rearrange("p m (b j) -> p m b j", j=ATOMS),
                 in1=weight_all[:, :, i, :].unsqueeze(1).to_broadcast([P, NF_TILES, MOLS, ATOMS]),
                 op=MULT,
             )
-            nc.scalar.activation(out=weighted[:], in_=weighted[:], func=mybir.ActivationFunctionType.Tanh)
-            nc.vector.tensor_reduce(out=sums_t[:, :, :, i], in_=weighted[:], axis=mybir.AxisListType.X, op=ADD)
 
-        first_end = PAIR * CHUNKS // RUN - 1 + LAG
-        atom_round = first_end + 1
+        def squash(i):
+            nc.scalar.activation(out=weighted[i][:], in_=weighted[i][:], func=mybir.ActivationFunctionType.Tanh)
+
+        def sum_over_j(i):
+            nc.vector.tensor_reduce(out=sums_t[:, :, :, i], in_=weighted[i][:], axis=mybir.AxisListType.X, op=ADD)
+
+        atom_round = CHUNKS + 2
         finished = []
+        with_bias = 0
         entered = 0
-        to_gate, to_flip = None, None
-        for n in range(ROUNDS + LAG + PAIR - 1 + 2):
-            to_finish, to_flip = to_flip, to_gate
-            fresh = range(RUN * n, RUN * n + RUN) if n < ROUNDS else ()
-            ripe = range(RUN * (n - LAG), RUN * (n - LAG) + RUN) if 0 <= n - LAG < ROUNDS else ()
+        late = [None] * LATE_STEPS
+        for batch in batches_of_round(0):
+            sort_batch(batch)
+        for n in range(ROUNDS + LAG + 1 + LATE_STEPS):
+            fresh = batches_of_round(n)
+            ripe = batches_of_round(n - LAG)
+            late = [None] + late[:-1]
+            if late[2] is not None:
+                quantise_gated(late[2])
+            if late[3] is not None:
+                weigh(late[3])
+            if late[4] is not None:
+                sum_over_j(late[4])
+            if n > atom_round and entered < with_bias:
+                late[0] = finished[entered]
+                entered += 1
+                gate(late[0])
+            for i in finished[with_bias:]:
+                add_bias(i)
+            with_bias = len(finished)
+            for batch in batches_of_round(n + 1):
+                sort_batch(batch)
             for batch in fresh:
                 transpose_batch(batch)
             if n == atom_round:
                 transpose_atoms()
-            if to_flip is not None:
-                transpose_gated(to_flip)
+            if late[1] is not None:
+                transpose_gated(late[1])
             for batch in ripe:
                 multiply_batch(batch)
-            if to_finish is not None:
-                multiply_gated(to_finish)
+                if batch_of(batch)[1] == CHUNKS - 1:
+                    finished.append(batch_of(batch)[0])
+            if late[2] is not None:
+                multiply_gated(late[2])
+            if 0 <= n - SPREAD_FROM < len(to_spread):
+                spread(*to_spread[n - SPREAD_FROM])
             for batch in fresh:
                 quantise_batch(batch)
-            for batch in ripe:
-                if batch_of(batch)[1] == CHUNKS - 1:
-                    add_bias(batch_of(batch)[0])
-                    finished.append(batch_of(batch)[0])
+            if late[1] is not None:
+                regroup_gated(late[1])
+            if late[3] is not None:
+                squash(late[3])
             if n == atom_round:
                 atom_hidden()
-            to_gate = None
-            if n >= atom_round and entered < len(finished):
-                to_gate = finished[entered]
-                entered += 1
-                gate(to_gate)
-            if to_flip is not None:
-                quantise_gated(to_flip)
-            if to_finish is not None:
-                sum_over_j(to_finish)
 
         final = late_bank.tile([P, NF_TILES, P], F32, name="late")
         for m in range(NF_TILES):

@@ -11,6 +11,7 @@ U8 = mybir.dt.uint8
 FP8X4 = mybir.dt.float8_e4m3fn_x4
 ADD = mybir.AluOpType.add
 MULT = mybir.AluOpType.mult
+TANH = mybir.ActivationFunctionType.Tanh
 
 P = 128
 PACK = 4
@@ -26,12 +27,7 @@ CHUNKS = GROUPS // CHUNK_GROUPS
 CHUNK_K = CHUNK_GROUPS * K_PASS
 BATCHES = ROW_TILES * CHUNKS
 BANK_GROUPS = 2
-RUN = 2
-LAG = 1
-ROUNDS = BATCHES // RUN
-assert RUN == PAIR
-LATE_STEPS = 5
-SPREAD_FROM = 2
+LAG = 2
 NF_TILES = NF // P
 PAIRS_OF_ATOMS = MOLS * ATOMS * ATOMS
 
@@ -40,16 +36,10 @@ FLOPS = 2 * PAIRS_OF_ATOMS * ND * NH + 2 * MOLS * ATOMS * NF * NH + 2 * PAIRS_OF
 
 def batch_of(n):
     if n < PAIR * CHUNKS:
-        c, i = divmod(n, PAIR)
+        c, j = divmod(n, PAIR)
     else:
-        i, c = divmod(n, CHUNKS)
-    return i, c
-
-
-def batches_of_round(n):
-    if 0 <= n < ROUNDS:
-        return range(RUN * n, RUN * n + RUN)
-    return range(0)
+        j, c = divmod(n, CHUNKS)
+    return j, c
 
 
 def tile_dtnnstep_pa_k_kernel(
@@ -70,15 +60,19 @@ def tile_dtnnstep_pa_k_kernel(
     with ExitStack() as stack:
         keep = stack.enter_context(tc.tile_pool(name="keep", bufs=1))
         work = stack.enter_context(tc.tile_pool(name="work", bufs=2))
-        operands = stack.enter_context(tc.tile_pool(name="operands", bufs=RUN * (LAG + 1)))
-        sorted_pool = stack.enter_context(tc.tile_pool(name="sorted_pool", bufs=RUN * 2))
+        operands = stack.enter_context(tc.tile_pool(name="operands", bufs=LAG + 2))
+        sorted_pool = stack.enter_context(tc.tile_pool(name="sorted_pool", bufs=4))
         sum_banks = stack.enter_context(tc.psum_pool(name="sum_banks", bufs=PAIR))
-        word_banks = stack.enter_context(tc.psum_pool(name="word_banks", bufs=RUN * CHUNK_GROUPS // BANK_GROUPS))
+        word_banks = stack.enter_context(tc.psum_pool(name="word_banks", bufs=4))
         flip_bank = stack.enter_context(tc.psum_pool(name="flip_bank", bufs=1))
         late_bank = stack.enter_context(tc.psum_pool(name="late_bank", bufs=1))
         stack.enter_context(tc.manual_schedule())
 
-        rows = keep.tile([P, 2 * NH + PAIRS_OF_ATOMS], BF16, name="rows")
+        df_planes = keep.tile([P, CHUNKS, NH], U8, name="df_planes", align_bytes=64)
+        fc_plane = keep.tile([P, NF], U8, name="fc_plane", align_bytes=64)
+        nc.vector.memset(df_planes[:].bitcast(I32), 0)
+        nc.vector.memset(fc_plane[:].bitcast(I32), 0)
+        rows = keep.tile([P, NH], BF16, name="rows")
         nc.vector.memset(rows[:].bitcast(I32), 0)
         ones = keep.tile([P, P], BF16, name="ones")
         nc.vector.memset(ones[:], 1.0)
@@ -87,17 +81,15 @@ def tile_dtnnstep_pa_k_kernel(
         ident_bf16 = keep.tile([P, P], BF16, name="ident_bf16")
         masks.make_identity(nc, ident_bf16[:])
 
-        df_planes = keep.tile([P, CHUNKS, NH], U8, name="df_planes", align_bytes=64)
-        fc_plane = keep.tile([P, NF], U8, name="fc_plane", align_bytes=64)
-        nc.vector.memset(df_planes[:].bitcast(I32), 0)
-        nc.vector.memset(fc_plane[:].bitcast(I32), 0)
-
+        pair_rows = distance_matrix.rearrange("b i j k -> (b i) j k")
         dist = {}
         df_words = {}
 
-        def load_distances(i, c):
-            dist[(i, c)] = keep.tile([P, CHUNK_K], BF16, name="dist_%d_%d" % (i, c))
-            nc.sync.dma_start(out=dist[(i, c)][:], in_=distance_matrix[:, i, :, c * CHUNK_K : (c + 1) * CHUNK_K])
+        def load_distances(n):
+            if n < BATCHES:
+                j, c = batch_of(n)
+                dist[n] = keep.tile([P, CHUNK_K], BF16, name="dist_%d" % n)
+                nc.sync.dma_start(out=dist[n][:], in_=pair_rows[:, j, c * CHUNK_K : (c + 1) * CHUNK_K])
 
         def load_df_words(c):
             df_words[c] = keep.tile([P, CHUNK_GROUPS, NH], U32, name="df_words_%d" % c, align_bytes=64)
@@ -107,58 +99,41 @@ def tile_dtnnstep_pa_k_kernel(
                 in_=groups.rearrange("g p n t -> p g (n t)").bitcast(I32),
             )
 
-        def load_round(n):
-            for batch in batches_of_round(n):
-                load_distances(*batch_of(batch))
-
-        load_round(0)
-        for c in range(CHUNKS):
-            load_round(c + 1)
-            if c == 0:
-                for chunk in range(CHUNKS):
-                    for quadrant in range(4):
-                        nc.sync.dma_start(
-                            out=df_planes[32 * quadrant : 32 * quadrant + 16, chunk, :].bitcast(I32),
-                            in_=W_df_scales[
-                                chunk * CHUNK_GROUPS : (chunk + 1) * CHUNK_GROUPS, 4 * quadrant : 4 * quadrant + 4, :
-                            ].bitcast(I32),
-                        )
-            load_df_words(c)
-            if c == 0:
-                nc.sync.dma_start(out=rows[0:1, 0:NH], in_=b_df.unsqueeze(0))
-                nc.sync.dma_start(out=rows[0:1, NH : 2 * NH], in_=b_cf.unsqueeze(0))
+        load_distances(0)
+        load_distances(1)
+        for chunk in range(CHUNKS):
+            for quadrant in range(4):
                 nc.sync.dma_start(
-                    out=rows[0:1, 2 * NH :], in_=distance_matrix_mask.rearrange("b i j -> (b i j)").unsqueeze(0)
+                    out=df_planes[32 * quadrant : 32 * quadrant + 16, chunk, :].bitcast(I32),
+                    in_=W_df_scales[
+                        chunk * CHUNK_GROUPS : (chunk + 1) * CHUNK_GROUPS, 4 * quadrant : 4 * quadrant + 4, :
+                    ].bitcast(I32),
                 )
-        load_round(CHUNKS + 1)
+        for c in range(CHUNKS):
+            load_df_words(c)
+            for s in range(PAIR):
+                load_distances(PAIR * (c + 1) + s)
         atoms = keep.tile([P, NF], BF16, name="atoms")
         nc.sync.dma_start(out=atoms[:], in_=atom_features.flatten_outer_dims())
-        cf_rows = keep.tile([P, NF // P, NH], BF16, name="cf_rows")
+        cf_rows = keep.tile([P, NF_TILES, NH], BF16, name="cf_rows")
         nc.sync.dma_start(out=cf_rows[:], in_=W_cf.rearrange("(c p) n -> p c n", p=P))
+        nc.sync.dma_start(out=rows[0:1, :], in_=b_df.unsqueeze(0))
+        bcf = keep.tile([P, PACK], BF16, name="bcf")
+        nc.sync.dma_start(out=bcf[:], in_=b_cf.rearrange("(p t) -> p t", t=PACK))
+        mask_bf16 = keep.tile([P, ATOMS], BF16, name="mask_bf16")
+        nc.sync.dma_start(out=mask_bf16[:], in_=distance_matrix_mask.rearrange("b i j -> (b i) j"))
         fc_words = keep.tile([P, NF], U32, name="fc_words", align_bytes=64)
         nc.sync.dma_start(
             out=fc_words[:].bitcast(I32), in_=W_fc_words[0].rearrange("p n t -> p (n t)").bitcast(I32)
         )
         for r in range(4):
             nc.sync.dma_start(out=fc_plane[r:P:32, :].bitcast(I32), in_=W_fc_scales[0, r:16:4, :].bitcast(I32))
-        for n in range(CHUNKS + 2, ROUNDS):
-            load_round(n)
-
-        bdf_all = keep.tile([P, NH], BF16, name="bdf_all")
-        weight_all = keep.tile([P, MOLS, ATOMS, ATOMS], BF16, name="weight_all")
-        weight_flat = weight_all[:].rearrange("p b i j -> p (b i j)")
-
-        def spread(columns, target):
-            bank = late_bank.tile([P, BANK], F32, name="late")
-            nc.tensor.matmul(out=bank[:], lhsT=ones[:], rhs=rows[:, columns], start=True, stop=True)
-            nc.vector.tensor_copy(out=target, in_=bank[:])
-
-        to_spread = [(slice(0, NH), bdf_all[:])]
-        for first in range(0, PAIRS_OF_ATOMS, BANK):
-            to_spread.append((slice(2 * NH + first, 2 * NH + first + BANK), weight_flat[:, first : first + BANK]))
+        for n in range(PAIR * (CHUNKS + 1), BATCHES):
+            load_distances(n)
 
         sorted_words = {}
         flipped = {}
+        grouped = {}
         quantised = {}
         sums = {}
 
@@ -166,7 +141,7 @@ def tile_dtnnstep_pa_k_kernel(
             sorted_words[n] = sorted_pool.tile([P, CHUNK_GROUPS, 2, P], F32, name="sorted_words")
             nc.vector.tensor_copy(
                 out=sorted_words[n][:],
-                in_=dist[batch_of(n)][:].bitcast(F32).rearrange("p (g w u) -> p g u w", g=CHUNK_GROUPS, u=2),
+                in_=dist[n][:].bitcast(F32).rearrange("p (g w u) -> p g u w", g=CHUNK_GROUPS, u=2),
             )
 
         def transpose_batch(n):
@@ -178,30 +153,32 @@ def tile_dtnnstep_pa_k_kernel(
                         nc.tensor.transpose(bank[:, s, u, :], sorted_words[n][:, first + s, u, :], ident_f32[:])
                 flipped[n].append(bank)
 
-        def quantise_batch(n):
-            grouped = work.tile([P, CHUNK_GROUPS, P, PACK], BF16, name="grouped", align_bytes=64)
-            codes = operands.tile([P, CHUNK_GROUPS, P], U32, name="codes", align_bytes=64)
-            scales = operands.tile([P, CHUNK_GROUPS, P], U8, name="scales", align_bytes=64)
+        def regroup_batch(n):
+            grouped[n] = work.tile([P, CHUNK_GROUPS, P, PACK], BF16, name="grouped", align_bytes=64)
             for first in range(0, CHUNK_GROUPS, BANK_GROUPS):
                 nc.scalar.copy(
-                    out=grouped[:, first : first + BANK_GROUPS].bitcast(F32),
+                    out=grouped[n][:, first : first + BANK_GROUPS].bitcast(F32),
                     in_=flipped[n][first // BANK_GROUPS][:].rearrange("p s u r -> p s r u"),
                 )
+
+        def quantise_batch(n):
+            codes = operands.tile([P, CHUNK_GROUPS, P], U32, name="codes", align_bytes=64)
+            scales = operands.tile([P, CHUNK_GROUPS, P], U8, name="scales", align_bytes=64)
             nc.vector.quantize_mx(
                 out=codes[:].rearrange("p s r -> p (s r)").bitcast(FP8X4),
                 scales=scales[:].rearrange("p s r -> p (s r)"),
-                in_=grouped[:].rearrange("p s r t -> p (s r t)"),
+                in_=grouped[n][:].rearrange("p s r t -> p (s r t)"),
             )
             quantised[n] = (codes, scales)
 
         def multiply_batch(n):
-            i, c = batch_of(n)
+            j, c = batch_of(n)
             codes, scales = quantised[n]
             if c == 0:
-                sums[i] = sum_banks.tile([P, NH], F32, name="dist_sum")
+                sums[j] = sum_banks.tile([P, NH], F32, name="dist_sum")
             for g in range(CHUNK_GROUPS):
                 nc.tensor.matmul_mx(
-                    out=sums[i][:],
+                    out=sums[j][:],
                     lhsT=codes[:, g, :].bitcast(FP8X4),
                     lhsT_scale=scales[:, g, :],
                     rhs=df_words[c][:, g, :].bitcast(FP8X4),
@@ -210,138 +187,144 @@ def tile_dtnnstep_pa_k_kernel(
                     stop=(c == CHUNKS - 1 and g == CHUNK_GROUPS - 1),
                 )
 
-        atom_h = keep.tile([P, NH], F32, name="atom_h")
-        atoms_t = keep.tile([P, NF // P, P], BF16, name="atoms_t")
-        atoms_flip = {}
+        bdf_all = keep.tile([P, PACK, P], BF16, name="bdf_all")
+        mask = keep.tile([P, ATOMS], F32, name="mask")
+        atoms_t = keep.tile([P, NF_TILES, P], BF16, name="atoms_t")
+        atom_h = keep.tile([P, ATOMS, MOLS, PACK], F32, name="atom_h")
+        small = {}
+
+        def spread_bias():
+            small["bias"] = late_bank.tile([P, BANK], F32, name="late")
+            nc.tensor.matmul(out=small["bias"][:], lhsT=ones[:], rhs=rows[:], start=True, stop=True)
+            nc.vector.tensor_copy(out=bdf_all[:], in_=small["bias"][:].rearrange("p (q t) -> p t q", t=PACK))
+            nc.vector.tensor_copy(out=mask[:], in_=mask_bf16[:])
 
         def transpose_atoms():
-            atoms_flip[0] = flip_bank.tile([P, NF // P, P], BF16, name="flip")
-            for c in range(NF // P):
-                nc.tensor.transpose(atoms_flip[0][:, c, :], atoms[:, c * P : (c + 1) * P], ident_bf16[:])
+            flip = flip_bank.tile([P, NF_TILES, P], BF16, name="flip")
+            for c in range(NF_TILES):
+                nc.tensor.transpose(flip[:, c, :], atoms[:, c * P : (c + 1) * P], ident_bf16[:])
+            nc.scalar.copy(out=atoms_t[:], in_=flip[:])
 
         def atom_hidden():
-            nc.scalar.copy(out=atoms_t[:], in_=atoms_flip[0][:])
-            product = late_bank.tile([P, NH], F32, name="late")
-            for c in range(NF // P):
-                nc.tensor.matmul(out=product[:], lhsT=atoms_t[:, c, :], rhs=cf_rows[:, c, :], start=(c == 0), stop=False)
-            nc.tensor.matmul(out=product[:], lhsT=ones[:], rhs=rows[:, NH : 2 * NH], start=False, stop=True)
-            nc.vector.tensor_copy(out=atom_h[:], in_=product[:])
+            product = late_bank.tile([P, PACK, P], F32, name="late")
+            for t in range(PACK):
+                for c in range(NF_TILES):
+                    nc.tensor.matmul(
+                        out=product[:, t, :],
+                        lhsT=cf_rows[:, c, t:NH:PACK],
+                        rhs=atoms_t[:, c, :],
+                        start=(c == 0),
+                        stop=(c == NF_TILES - 1),
+                    )
+            nc.vector.tensor_tensor(
+                out=atom_h[:],
+                in0=product[:].rearrange("p t (b j) -> p j b t", j=ATOMS),
+                in1=bcf[:].unsqueeze(1).unsqueeze(1).to_broadcast([P, ATOMS, MOLS, PACK]),
+                op=ADD,
+            )
 
         biased = {}
+        hidden_t = {}
         gated = {}
-        gated_flip = {}
-        gated_grouped = {}
         gated_mx = {}
         products = {}
-        weighted = {}
-        sums_t = keep.tile([P, NF_TILES, MOLS, ATOMS], F32, name="sums_t")
+        squashed = {}
+        totals = {}
 
-        def add_bias(i):
-            biased[i] = work.tile([P, NH], F32, name="biased")
-            nc.vector.tensor_tensor(out=biased[i][:], in0=sums[i][:], in1=bdf_all[:], op=ADD)
-
-        def gate(i):
-            gated[i] = work.tile([P, NH], BF16, name="gated")
-            nc.vector.tensor_tensor(out=gated[i][:], in0=biased[i][:], in1=atom_h[:], op=MULT)
-
-        def transpose_gated(i):
-            gated_flip[i] = flip_bank.tile([P, PACK, P], BF16, name="flip")
-            for t in range(PACK):
-                nc.tensor.transpose(gated_flip[i][:, t, :], gated[i][:, t:NH:PACK], ident_bf16[:])
-
-        def regroup_gated(i):
-            gated_grouped[i] = work.tile([P, P, PACK], BF16, name="gated_grouped", align_bytes=64)
-            nc.scalar.copy(out=gated_grouped[i][:], in_=gated_flip[i][:].rearrange("p t r -> p r t"))
-
-        def quantise_gated(i):
-            codes = work.tile([P, P], U32, name="gated_codes", align_bytes=64)
-            scales = work.tile([P, P], U8, name="gated_scales", align_bytes=64)
-            nc.vector.quantize_mx(
-                out=codes[:].bitcast(FP8X4), scales=scales[:], in_=gated_grouped[i][:].rearrange("p r t -> p (r t)")
-            )
-            gated_mx[i] = (codes, scales)
-
-        def multiply_gated(i):
-            codes, scales = gated_mx[i]
-            products[i] = late_bank.tile([P, NF_TILES, P], F32, name="late")
-            for m in range(NF_TILES):
-                nc.tensor.matmul_mx(
-                    out=products[i][:, m, :],
-                    lhsT=fc_words[:, m * P : (m + 1) * P].bitcast(FP8X4),
-                    lhsT_scale=fc_plane[:, m * P : (m + 1) * P],
-                    rhs=codes[:].bitcast(FP8X4),
-                    rhs_scale=scales[:],
-                    start=True,
-                    stop=True,
-                )
-
-        def weigh(i):
-            weighted[i] = work.tile([P, NF_TILES, MOLS, ATOMS], F32, name="weighted")
+        def add_bias(j):
+            biased[j] = work.tile([P, PACK, P], F32, name="biased")
             nc.vector.tensor_tensor(
-                out=weighted[i][:],
-                in0=products[i][:].rearrange("p m (b j) -> p m b j", j=ATOMS),
-                in1=weight_all[:, :, i, :].unsqueeze(1).to_broadcast([P, NF_TILES, MOLS, ATOMS]),
+                out=biased[j][:], in0=sums[j][:].rearrange("p (q t) -> p t q", t=PACK), in1=bdf_all[:], op=ADD
+            )
+
+        def transpose_hidden(j):
+            hidden_t[j] = flip_bank.tile([P, PACK, P], F32, name="flip")
+            for t in range(PACK):
+                nc.tensor.transpose(hidden_t[j][:, t, :], biased[j][:, t, :], ident_f32[:])
+
+        def gate(j):
+            gated[j] = work.tile([P, MOLS, ATOMS, PACK], BF16, name="gated", align_bytes=64)
+            nc.vector.tensor_tensor(
+                out=gated[j][:],
+                in0=hidden_t[j][:].rearrange("p t (b i) -> p b i t", i=ATOMS),
+                in1=atom_h[:, j].unsqueeze(2).to_broadcast([P, MOLS, ATOMS, PACK]),
                 op=MULT,
             )
 
-        def squash(i):
-            nc.scalar.activation(out=weighted[i][:], in_=weighted[i][:], func=mybir.ActivationFunctionType.Tanh)
+        def quantise_gated(j):
+            codes = work.tile([P, P], U32, name="gated_codes", align_bytes=64)
+            scales = work.tile([P, P], U8, name="gated_scales", align_bytes=64)
+            nc.vector.quantize_mx(
+                out=codes[:].bitcast(FP8X4), scales=scales[:], in_=gated[j][:].rearrange("p b i t -> p (b i t)")
+            )
+            gated_mx[j] = (codes, scales)
 
-        def sum_over_j(i):
-            nc.vector.tensor_reduce(out=sums_t[:, :, :, i], in_=weighted[i][:], axis=mybir.AxisListType.X, op=ADD)
+        def multiply_gated(j):
+            codes, scales = gated_mx[j]
+            products[j] = late_bank.tile([P, NF], F32, name="late")
+            nc.tensor.matmul_mx(
+                out=products[j][:],
+                lhsT=codes[:].bitcast(FP8X4),
+                lhsT_scale=scales[:],
+                rhs=fc_words[:].bitcast(FP8X4),
+                rhs_scale=fc_plane[:],
+                start=True,
+                stop=True,
+            )
 
-        atom_round = CHUNKS + 2
-        finished = []
-        with_bias = 0
-        entered = 0
-        late = [None] * LATE_STEPS
-        for batch in batches_of_round(0):
-            sort_batch(batch)
-        for n in range(ROUNDS + LAG + 1 + LATE_STEPS):
-            fresh = batches_of_round(n)
-            ripe = batches_of_round(n - LAG)
-            late = [None] + late[:-1]
-            if late[2] is not None:
-                quantise_gated(late[2])
-            if late[3] is not None:
-                weigh(late[3])
-            if late[4] is not None:
-                sum_over_j(late[4])
-            if n > atom_round and entered < with_bias:
-                late[0] = finished[entered]
-                entered += 1
-                gate(late[0])
-            for i in finished[with_bias:]:
-                add_bias(i)
-            with_bias = len(finished)
-            for batch in batches_of_round(n + 1):
-                sort_batch(batch)
-            for batch in fresh:
-                transpose_batch(batch)
-            if n == atom_round:
+        def squash(j):
+            squashed[j] = work.tile([P, NF], F32, name="squashed")
+            nc.scalar.activation(out=squashed[j][:], in_=products[j][:], func=TANH, scale=mask[:, j : j + 1])
+
+        def accumulate(j):
+            previous = atoms if j == 0 else totals[j - 1]
+            totals[j] = work.tile([P, NF], F32, name="total")
+            nc.vector.tensor_tensor(out=totals[j][:], in0=squashed[j][:], in1=previous[:], op=ADD)
+
+        SMALL_STEP = PAIR * CHUNKS
+        stage = {}
+        for n in range(BATCHES):
+            j, c = batch_of(n)
+            if c == CHUNKS - 1:
+                first = max(n + LAG + 1, SMALL_STEP + 2)
+                if j > 0:
+                    first = max(first, start_step + 1)
+                start_step = first
+                for s in range(5):
+                    stage[(s, first + s)] = j
+                last_step = first + 4
+        for n in range(2):
+            sort_batch(n)
+        for n in range(last_step + 1):
+            if 0 <= n - 1 < BATCHES:
+                quantise_batch(n - 1)
+            if (0, n) in stage:
+                add_bias(stage[(0, n)])
+            if (2, n) in stage:
+                quantise_gated(stage[(2, n)])
+            if n + 2 < BATCHES:
+                sort_batch(n + 2)
+            if (4, n) in stage:
+                accumulate(stage[(4, n)])
+            if (3, n) in stage:
+                squash(stage[(3, n)])
+            if n < BATCHES:
+                transpose_batch(n)
+            if (1, n) in stage:
+                transpose_hidden(stage[(1, n)])
+            if n == SMALL_STEP:
                 transpose_atoms()
-            if late[1] is not None:
-                transpose_gated(late[1])
-            for batch in ripe:
-                multiply_batch(batch)
-                if batch_of(batch)[1] == CHUNKS - 1:
-                    finished.append(batch_of(batch)[0])
-            if late[2] is not None:
-                multiply_gated(late[2])
-            if 0 <= n - SPREAD_FROM < len(to_spread):
-                spread(*to_spread[n - SPREAD_FROM])
-            for batch in fresh:
-                quantise_batch(batch)
-            if late[1] is not None:
-                regroup_gated(late[1])
-            if late[3] is not None:
-                squash(late[3])
-            if n == atom_round:
+            if 0 <= n - LAG < BATCHES:
+                multiply_batch(n - LAG)
+            if (2, n) in stage:
+                multiply_gated(stage[(2, n)])
+            if n == SMALL_STEP:
+                spread_bias()
+            if n == SMALL_STEP + 1:
                 atom_hidden()
+            if n < BATCHES:
+                regroup_batch(n)
+            if (1, n) in stage:
+                gate(stage[(1, n)])
 
-        final = late_bank.tile([P, NF_TILES, P], F32, name="late")
-        for m in range(NF_TILES):
-            nc.tensor.transpose(final[:, m, :], sums_t[:, m].rearrange("p b i -> p (b i)"), ident_f32[:])
-        result = keep.tile([P, NF], F32, name="result")
-        nc.vector.tensor_tensor(out=result[:], in0=final[:].rearrange("p m f -> p (m f)"), in1=atoms[:], op=ADD)
-        nc.sync.dma_start(out=out.flatten_outer_dims(), in_=result[:])
+        nc.sync.dma_start(out=out.flatten_outer_dims(), in_=totals[ROW_TILES - 1][:])

@@ -21,12 +21,14 @@ MOLS, ATOMS = 16, 8
 NF, ND, NH = 512, 8192, 512
 GROUPS = ND // K_PASS
 ROW_TILES = ATOMS
-PAIR = 2
+FIRST_TILES = 3
 CHUNK_GROUPS = 4
 CHUNKS = GROUPS // CHUNK_GROUPS
 CHUNK_K = CHUNK_GROUPS * K_PASS
 BATCHES = ROW_TILES * CHUNKS
 BANK_GROUPS = 2
+EARLY = 4
+AHEAD = 2
 LAG = 2
 NF_TILES = NF // P
 PAIRS_OF_ATOMS = MOLS * ATOMS * ATOMS
@@ -35,11 +37,15 @@ FLOPS = 2 * PAIRS_OF_ATOMS * ND * NH + 2 * MOLS * ATOMS * NF * NH + 2 * PAIRS_OF
 
 
 def batch_of(n):
-    if n < PAIR * CHUNKS:
-        c, j = divmod(n, PAIR)
+    if n < FIRST_TILES * CHUNKS:
+        c, j = divmod(n, FIRST_TILES)
     else:
         j, c = divmod(n, CHUNKS)
     return j, c
+
+
+def step_of_passes(n):
+    return n + 1 if n < EARLY - 1 else n + LAG
 
 
 def tile_dtnnstep_pa_k_kernel(
@@ -62,10 +68,8 @@ def tile_dtnnstep_pa_k_kernel(
         work = stack.enter_context(tc.tile_pool(name="work", bufs=2))
         operands = stack.enter_context(tc.tile_pool(name="operands", bufs=LAG + 2))
         sorted_pool = stack.enter_context(tc.tile_pool(name="sorted_pool", bufs=4))
-        sum_banks = stack.enter_context(tc.psum_pool(name="sum_banks", bufs=PAIR))
+        banks = stack.enter_context(tc.psum_pool(name="banks", bufs=1))
         word_banks = stack.enter_context(tc.psum_pool(name="word_banks", bufs=4))
-        flip_bank = stack.enter_context(tc.psum_pool(name="flip_bank", bufs=1))
-        late_bank = stack.enter_context(tc.psum_pool(name="late_bank", bufs=1))
         stack.enter_context(tc.manual_schedule())
 
         df_planes = keep.tile([P, CHUNKS, NH], U8, name="df_planes", align_bytes=64)
@@ -86,10 +90,9 @@ def tile_dtnnstep_pa_k_kernel(
         df_words = {}
 
         def load_distances(n):
-            if n < BATCHES:
-                j, c = batch_of(n)
-                dist[n] = keep.tile([P, CHUNK_K], BF16, name="dist_%d" % n)
-                nc.sync.dma_start(out=dist[n][:], in_=pair_rows[:, j, c * CHUNK_K : (c + 1) * CHUNK_K])
+            j, c = batch_of(n)
+            dist[n] = keep.tile([P, CHUNK_K], BF16, name="dist_%d" % n)
+            nc.sync.dma_start(out=dist[n][:], in_=pair_rows[:, j, c * CHUNK_K : (c + 1) * CHUNK_K])
 
         def load_df_words(c):
             df_words[c] = keep.tile([P, CHUNK_GROUPS, NH], U32, name="df_words_%d" % c, align_bytes=64)
@@ -99,20 +102,27 @@ def tile_dtnnstep_pa_k_kernel(
                 in_=groups.rearrange("g p n t -> p g (n t)").bitcast(I32),
             )
 
+        def load_df_scales(chunks):
+            for chunk in chunks:
+                for quadrant in range(4):
+                    nc.sync.dma_start(
+                        out=df_planes[32 * quadrant : 32 * quadrant + 16, chunk, :].bitcast(I32),
+                        in_=W_df_scales[
+                            chunk * CHUNK_GROUPS : (chunk + 1) * CHUNK_GROUPS, 4 * quadrant : 4 * quadrant + 4, :
+                        ].bitcast(I32),
+                    )
+
         load_distances(0)
         load_distances(1)
-        for chunk in range(CHUNKS):
-            for quadrant in range(4):
-                nc.sync.dma_start(
-                    out=df_planes[32 * quadrant : 32 * quadrant + 16, chunk, :].bitcast(I32),
-                    in_=W_df_scales[
-                        chunk * CHUNK_GROUPS : (chunk + 1) * CHUNK_GROUPS, 4 * quadrant : 4 * quadrant + 4, :
-                    ].bitcast(I32),
-                )
         for c in range(CHUNKS):
+            if c == 0:
+                load_df_scales([0])
             load_df_words(c)
-            for s in range(PAIR):
-                load_distances(PAIR * (c + 1) + s)
+            for n in range(FIRST_TILES * c + 2, FIRST_TILES * (c + 1) + 2):
+                if n < FIRST_TILES * CHUNKS:
+                    load_distances(n)
+            if c == 0:
+                load_df_scales(range(1, CHUNKS))
         atoms = keep.tile([P, NF], BF16, name="atoms")
         nc.sync.dma_start(out=atoms[:], in_=atom_features.flatten_outer_dims())
         cf_rows = keep.tile([P, NF_TILES, NH], BF16, name="cf_rows")
@@ -128,7 +138,7 @@ def tile_dtnnstep_pa_k_kernel(
         )
         for r in range(4):
             nc.sync.dma_start(out=fc_plane[r:P:32, :].bitcast(I32), in_=W_fc_scales[0, r:16:4, :].bitcast(I32))
-        for n in range(PAIR * (CHUNKS + 1), BATCHES):
+        for n in range(FIRST_TILES * CHUNKS, BATCHES):
             load_distances(n)
 
         sorted_words = {}
@@ -175,7 +185,7 @@ def tile_dtnnstep_pa_k_kernel(
             j, c = batch_of(n)
             codes, scales = quantised[n]
             if c == 0:
-                sums[j] = sum_banks.tile([P, NH], F32, name="dist_sum")
+                sums[j] = banks.tile([P, NH], F32, name="bank_%d" % (j if j < FIRST_TILES else (j - FIRST_TILES) % 2))
             for g in range(CHUNK_GROUPS):
                 nc.tensor.matmul_mx(
                     out=sums[j][:],
@@ -194,19 +204,19 @@ def tile_dtnnstep_pa_k_kernel(
         small = {}
 
         def spread_bias():
-            small["bias"] = late_bank.tile([P, BANK], F32, name="late")
+            small["bias"] = banks.tile([P, BANK], F32, name="bank_flip")
             nc.tensor.matmul(out=small["bias"][:], lhsT=ones[:], rhs=rows[:], start=True, stop=True)
             nc.vector.tensor_copy(out=bdf_all[:], in_=small["bias"][:].rearrange("p (q t) -> p t q", t=PACK))
             nc.vector.tensor_copy(out=mask[:], in_=mask_bf16[:])
 
         def transpose_atoms():
-            flip = flip_bank.tile([P, NF_TILES, P], BF16, name="flip")
+            flip = banks.tile([P, NF_TILES, P], BF16, name="bank_flip")
             for c in range(NF_TILES):
                 nc.tensor.transpose(flip[:, c, :], atoms[:, c * P : (c + 1) * P], ident_bf16[:])
             nc.scalar.copy(out=atoms_t[:], in_=flip[:])
 
         def atom_hidden():
-            product = late_bank.tile([P, PACK, P], F32, name="late")
+            product = banks.tile([P, PACK, P], F32, name="bank_flip")
             for t in range(PACK):
                 for c in range(NF_TILES):
                     nc.tensor.matmul(
@@ -238,7 +248,7 @@ def tile_dtnnstep_pa_k_kernel(
             )
 
         def transpose_hidden(j):
-            hidden_t[j] = flip_bank.tile([P, PACK, P], F32, name="flip")
+            hidden_t[j] = banks.tile([P, PACK, P], F32, name="bank_flip")
             for t in range(PACK):
                 nc.tensor.transpose(hidden_t[j][:, t, :], biased[j][:, t, :], ident_f32[:])
 
@@ -261,7 +271,7 @@ def tile_dtnnstep_pa_k_kernel(
 
         def multiply_gated(j):
             codes, scales = gated_mx[j]
-            products[j] = late_bank.tile([P, NF], F32, name="late")
+            products[j] = banks.tile([P, NF], F32, name="bank_2")
             nc.tensor.matmul_mx(
                 out=products[j][:],
                 lhsT=codes[:].bitcast(FP8X4),
@@ -281,29 +291,27 @@ def tile_dtnnstep_pa_k_kernel(
             totals[j] = work.tile([P, NF], F32, name="total")
             nc.vector.tensor_tensor(out=totals[j][:], in0=squashed[j][:], in1=previous[:], op=ADD)
 
-        SMALL_STEP = PAIR * CHUNKS
+        SMALL_STEP = FIRST_TILES * (CHUNKS - 1)
+        passes = {}
         stage = {}
         for n in range(BATCHES):
+            passes.setdefault(step_of_passes(n), []).append(n)
             j, c = batch_of(n)
             if c == CHUNKS - 1:
-                first = max(n + LAG + 1, SMALL_STEP + 2)
-                if j > 0:
-                    first = max(first, start_step + 1)
-                start_step = first
                 for s in range(5):
-                    stage[(s, first + s)] = j
-                last_step = first + 4
-        for n in range(2):
-            sort_batch(n)
-        for n in range(last_step + 1):
+                    stage[(s, step_of_passes(n) + 1 + s)] = j
+        ready = 0
+        for n in range(step_of_passes(BATCHES - 1) + 6):
             if 0 <= n - 1 < BATCHES:
                 quantise_batch(n - 1)
             if (0, n) in stage:
                 add_bias(stage[(0, n)])
             if (2, n) in stage:
                 quantise_gated(stage[(2, n)])
-            if n + 2 < BATCHES:
-                sort_batch(n + 2)
+            target = n + 2 if n < EARLY else n + 1 + AHEAD
+            for batch in range(ready, min(target, BATCHES)):
+                sort_batch(batch)
+            ready = target
             if (4, n) in stage:
                 accumulate(stage[(4, n)])
             if (3, n) in stage:
@@ -312,15 +320,15 @@ def tile_dtnnstep_pa_k_kernel(
                 transpose_batch(n)
             if (1, n) in stage:
                 transpose_hidden(stage[(1, n)])
-            if n == SMALL_STEP:
+            if n == SMALL_STEP + 1:
                 transpose_atoms()
-            if 0 <= n - LAG < BATCHES:
-                multiply_batch(n - LAG)
+            for batch in passes.get(n, []):
+                multiply_batch(batch)
             if (2, n) in stage:
                 multiply_gated(stage[(2, n)])
             if n == SMALL_STEP:
                 spread_bias()
-            if n == SMALL_STEP + 1:
+            if n == SMALL_STEP + 2:
                 atom_hidden()
             if n < BATCHES:
                 regroup_batch(n)

@@ -27,9 +27,11 @@ CHUNKS = GROUPS // CHUNK_GROUPS
 CHUNK_K = CHUNK_GROUPS * K_PASS
 BATCHES = ROW_TILES * CHUNKS
 BANK_GROUPS = 2
-EARLY = 4
-AHEAD = 2
-LAG = 2
+BATCH_BANKS = CHUNK_GROUPS // BANK_GROUPS
+UNITS = BATCHES * BATCH_BANKS
+WORD_BANKS = 4
+FIRST_ROUNDS = 4
+RUN = 3
 NF_TILES = NF // P
 PAIRS_OF_ATOMS = MOLS * ATOMS * ATOMS
 
@@ -44,8 +46,14 @@ def batch_of(n):
     return j, c
 
 
-def step_of_passes(n):
-    return n + 1 if n < EARLY - 1 else n + LAG
+def rounds_of_units():
+    rounds = []
+    first = 0
+    while first < UNITS:
+        size = BATCH_BANKS if len(rounds) < FIRST_ROUNDS else RUN
+        rounds.append(list(range(first, min(first + size, UNITS))))
+        first += size
+    return rounds
 
 
 def tile_dtnnstep_pa_k_kernel(
@@ -66,10 +74,11 @@ def tile_dtnnstep_pa_k_kernel(
     with ExitStack() as stack:
         keep = stack.enter_context(tc.tile_pool(name="keep", bufs=1))
         work = stack.enter_context(tc.tile_pool(name="work", bufs=2))
-        operands = stack.enter_context(tc.tile_pool(name="operands", bufs=LAG + 2))
+        operands = stack.enter_context(tc.tile_pool(name="operands", bufs=3 * RUN))
         sorted_pool = stack.enter_context(tc.tile_pool(name="sorted_pool", bufs=4))
+        grouped_pool = stack.enter_context(tc.tile_pool(name="grouped_pool", bufs=WORD_BANKS))
         banks = stack.enter_context(tc.psum_pool(name="banks", bufs=1))
-        word_banks = stack.enter_context(tc.psum_pool(name="word_banks", bufs=4))
+        word_banks = stack.enter_context(tc.psum_pool(name="word_banks", bufs=WORD_BANKS))
         stack.enter_context(tc.manual_schedule())
 
         df_planes = keep.tile([P, CHUNKS, NH], U8, name="df_planes", align_bytes=64)
@@ -151,46 +160,48 @@ def tile_dtnnstep_pa_k_kernel(
             sorted_words[n] = sorted_pool.tile([P, CHUNK_GROUPS, 2, P], F32, name="sorted_words")
             nc.vector.tensor_copy(
                 out=sorted_words[n][:],
-                in_=dist[n][:].bitcast(F32).rearrange("p (g w u) -> p g u w", g=CHUNK_GROUPS, u=2),
+                in_=dist[n][:].bitcast(F32).rearrange("p (g w h) -> p g h w", g=CHUNK_GROUPS, h=2),
             )
 
-        def transpose_batch(n):
-            flipped[n] = []
-            for first in range(0, CHUNK_GROUPS, BANK_GROUPS):
-                bank = word_banks.tile([P, BANK_GROUPS, 2, P], F32, name="bank")
-                for s in range(BANK_GROUPS):
-                    for u in range(2):
-                        nc.tensor.transpose(bank[:, s, u, :], sorted_words[n][:, first + s, u, :], ident_f32[:])
-                flipped[n].append(bank)
+        def transpose_unit(u):
+            n, part = divmod(u, BATCH_BANKS)
+            flipped[u] = word_banks.tile([P, BANK_GROUPS, 2, P], F32, name="bank")
+            for s in range(BANK_GROUPS):
+                for half in range(2):
+                    nc.tensor.transpose(
+                        flipped[u][:, s, half, :],
+                        sorted_words[n][:, part * BANK_GROUPS + s, half, :],
+                        ident_f32[:],
+                    )
 
-        def regroup_batch(n):
-            grouped[n] = work.tile([P, CHUNK_GROUPS, P, PACK], BF16, name="grouped", align_bytes=64)
-            for first in range(0, CHUNK_GROUPS, BANK_GROUPS):
-                nc.scalar.copy(
-                    out=grouped[n][:, first : first + BANK_GROUPS].bitcast(F32),
-                    in_=flipped[n][first // BANK_GROUPS][:].rearrange("p s u r -> p s r u"),
-                )
+        def regroup_unit(u):
+            grouped[u] = grouped_pool.tile([P, BANK_GROUPS, P, PACK], BF16, name="grouped", align_bytes=64)
+            nc.scalar.copy(out=grouped[u][:].bitcast(F32), in_=flipped[u][:].rearrange("p s h r -> p s r h"))
 
-        def quantise_batch(n):
-            codes = operands.tile([P, CHUNK_GROUPS, P], U32, name="codes", align_bytes=64)
-            scales = operands.tile([P, CHUNK_GROUPS, P], U8, name="scales", align_bytes=64)
+        def quantise_unit(u):
+            codes = operands.tile([P, BANK_GROUPS, P], U32, name="codes", align_bytes=64)
+            scales = operands.tile([P, BANK_GROUPS, P], U8, name="scales", align_bytes=64)
             nc.vector.quantize_mx(
                 out=codes[:].rearrange("p s r -> p (s r)").bitcast(FP8X4),
                 scales=scales[:].rearrange("p s r -> p (s r)"),
-                in_=grouped[n][:].rearrange("p s r t -> p (s r t)"),
+                in_=grouped[u][:].rearrange("p s r t -> p (s r t)"),
             )
-            quantised[n] = (codes, scales)
+            quantised[u] = (codes, scales)
 
-        def multiply_batch(n):
+        def multiply_unit(u):
+            n, part = divmod(u, BATCH_BANKS)
             j, c = batch_of(n)
-            codes, scales = quantised[n]
-            if c == 0:
-                sums[j] = banks.tile([P, NH], F32, name="bank_%d" % (j if j < FIRST_TILES else (j - FIRST_TILES) % 2))
-            for g in range(CHUNK_GROUPS):
+            codes, scales = quantised[u]
+            if c == 0 and part == 0:
+                sums[j] = banks.tile(
+                    [P, NH], F32, name="bank_%d" % (j if j < FIRST_TILES else (j - FIRST_TILES) % 2)
+                )
+            for s in range(BANK_GROUPS):
+                g = part * BANK_GROUPS + s
                 nc.tensor.matmul_mx(
                     out=sums[j][:],
-                    lhsT=codes[:, g, :].bitcast(FP8X4),
-                    lhsT_scale=scales[:, g, :],
+                    lhsT=codes[:, s, :].bitcast(FP8X4),
+                    lhsT_scale=scales[:, s, :],
                     rhs=df_words[c][:, g, :].bitcast(FP8X4),
                     rhs_scale=df_planes[PACK * g : P, c, :],
                     start=(c == 0 and g == 0),
@@ -291,48 +302,57 @@ def tile_dtnnstep_pa_k_kernel(
             totals[j] = work.tile([P, NF], F32, name="total")
             nc.vector.tensor_tensor(out=totals[j][:], in0=squashed[j][:], in1=previous[:], op=ADD)
 
-        SMALL_STEP = FIRST_TILES * (CHUNKS - 1)
-        passes = {}
+        rounds = rounds_of_units()
+        SMALL_ROUND = 7
         stage = {}
-        for n in range(BATCHES):
-            passes.setdefault(step_of_passes(n), []).append(n)
-            j, c = batch_of(n)
-            if c == CHUNKS - 1:
-                for s in range(5):
-                    stage[(s, step_of_passes(n) + 1 + s)] = j
-        ready = 0
-        for n in range(step_of_passes(BATCHES - 1) + 6):
-            if 0 <= n - 1 < BATCHES:
-                quantise_batch(n - 1)
-            if (0, n) in stage:
-                add_bias(stage[(0, n)])
-            if (2, n) in stage:
-                quantise_gated(stage[(2, n)])
-            target = n + 2 if n < EARLY else n + 1 + AHEAD
-            for batch in range(ready, min(target, BATCHES)):
-                sort_batch(batch)
-            ready = target
-            if (4, n) in stage:
-                accumulate(stage[(4, n)])
-            if (3, n) in stage:
-                squash(stage[(3, n)])
-            if n < BATCHES:
-                transpose_batch(n)
-            if (1, n) in stage:
-                transpose_hidden(stage[(1, n)])
-            if n == SMALL_STEP + 1:
+        start = 0
+        for m in range(len(rounds)):
+            for u in rounds[m]:
+                n, part = divmod(u, BATCH_BANKS)
+                j, c = batch_of(n)
+                if c == CHUNKS - 1 and part == BATCH_BANKS - 1:
+                    start = max(start + 1, m + 2)
+                    for s in range(5):
+                        stage[(s, start + s)] = j
+        assert stage[(0, SMALL_ROUND + 2)] == 0
+
+        def sort_round(m):
+            if m < len(rounds):
+                for u in rounds[m]:
+                    if u % BATCH_BANKS == 0:
+                        sort_batch(u // BATCH_BANKS)
+
+        sort_round(0)
+        for m in range(start + 5):
+            fresh = rounds[m] if m < len(rounds) else []
+            ripe = rounds[m - 1] if 0 <= m - 1 < len(rounds) else []
+            sort_round(m + 1)
+            if (0, m) in stage:
+                add_bias(stage[(0, m)])
+            if (2, m) in stage:
+                quantise_gated(stage[(2, m)])
+            if (3, m) in stage:
+                squash(stage[(3, m)])
+            if (4, m) in stage:
+                accumulate(stage[(4, m)])
+            for u in fresh:
+                transpose_unit(u)
+            if (1, m) in stage:
+                transpose_hidden(stage[(1, m)])
+            if m == SMALL_ROUND + 1:
                 transpose_atoms()
-            for batch in passes.get(n, []):
-                multiply_batch(batch)
-            if (2, n) in stage:
-                multiply_gated(stage[(2, n)])
-            if n == SMALL_STEP:
+            for u in ripe:
+                multiply_unit(u)
+            if (2, m) in stage:
+                multiply_gated(stage[(2, m)])
+            if m == SMALL_ROUND:
                 spread_bias()
-            if n == SMALL_STEP + 2:
+            if m == SMALL_ROUND + 2:
                 atom_hidden()
-            if n < BATCHES:
-                regroup_batch(n)
-            if (1, n) in stage:
-                gate(stage[(1, n)])
+            for u in fresh:
+                regroup_unit(u)
+                quantise_unit(u)
+            if (1, m) in stage:
+                gate(stage[(1, m)])
 
         nc.sync.dma_start(out=out.flatten_outer_dims(), in_=totals[ROW_TILES - 1][:])

@@ -21,28 +21,29 @@ MOLS, ATOMS = 16, 8
 NF, ND, NH = 512, 8192, 512
 GROUPS = ND // K_PASS
 ROW_TILES = ATOMS
-FIRST_TILES = 3
-CHUNK_GROUPS = 4
-CHUNKS = GROUPS // CHUNK_GROUPS
-CHUNK_K = CHUNK_GROUPS * K_PASS
-BATCHES = ROW_TILES * CHUNKS
-BANK_GROUPS = 2
-BATCH_BANKS = CHUNK_GROUPS // BANK_GROUPS
-UNITS = BATCHES * BATCH_BANKS
+FIRST_TILES = 4
+PLANE_GROUPS = 4
+UNIT_GROUPS = 2
+UNIT_K = UNIT_GROUPS * K_PASS
+STRIPS = GROUPS // UNIT_GROUPS
+UNITS = ROW_TILES * STRIPS
+FIRST_UNITS = FIRST_TILES * STRIPS
+LOAD_UNITS = 2
 WORD_BANKS = 4
 FIRST_ROUNDS = 4
 RUN = 3
+SMALL_ROUND = 10
 NF_TILES = NF // P
 PAIRS_OF_ATOMS = MOLS * ATOMS * ATOMS
 
 FLOPS = 2 * PAIRS_OF_ATOMS * ND * NH + 2 * MOLS * ATOMS * NF * NH + 2 * PAIRS_OF_ATOMS * NH * NF
 
 
-def batch_of(n):
-    if n < FIRST_TILES * CHUNKS:
-        c, j = divmod(n, FIRST_TILES)
+def unit_of(u):
+    if u < FIRST_UNITS:
+        c, j = divmod(u, FIRST_TILES)
     else:
-        j, c = divmod(n, CHUNKS)
+        j, c = divmod(u, STRIPS)
     return j, c
 
 
@@ -50,7 +51,7 @@ def rounds_of_units():
     rounds = []
     first = 0
     while first < UNITS:
-        size = BATCH_BANKS if len(rounds) < FIRST_ROUNDS else RUN
+        size = 1 if len(rounds) < FIRST_ROUNDS else RUN
         rounds.append(list(range(first, min(first + size, UNITS))))
         first += size
     return rounds
@@ -74,14 +75,15 @@ def tile_dtnnstep_pa_k_kernel(
     with ExitStack() as stack:
         keep = stack.enter_context(tc.tile_pool(name="keep", bufs=1))
         work = stack.enter_context(tc.tile_pool(name="work", bufs=2))
-        operands = stack.enter_context(tc.tile_pool(name="operands", bufs=3 * RUN))
-        sorted_pool = stack.enter_context(tc.tile_pool(name="sorted_pool", bufs=4))
+        operands = stack.enter_context(tc.tile_pool(name="operands", bufs=2 * RUN + 2))
+        sorted_pool = stack.enter_context(tc.tile_pool(name="sorted_pool", bufs=2 * RUN + 2))
+        biased_pool = stack.enter_context(tc.tile_pool(name="biased_pool", bufs=FIRST_TILES))
         grouped_pool = stack.enter_context(tc.tile_pool(name="grouped_pool", bufs=WORD_BANKS))
         banks = stack.enter_context(tc.psum_pool(name="banks", bufs=1))
         word_banks = stack.enter_context(tc.psum_pool(name="word_banks", bufs=WORD_BANKS))
         stack.enter_context(tc.manual_schedule())
 
-        df_planes = keep.tile([P, CHUNKS, NH], U8, name="df_planes", align_bytes=64)
+        df_planes = keep.tile([P, GROUPS // PLANE_GROUPS, NH], U8, name="df_planes", align_bytes=64)
         fc_plane = keep.tile([P, NF], U8, name="fc_plane", align_bytes=64)
         nc.vector.memset(df_planes[:].bitcast(I32), 0)
         nc.vector.memset(fc_plane[:].bitcast(I32), 0)
@@ -94,61 +96,80 @@ def tile_dtnnstep_pa_k_kernel(
         ident_bf16 = keep.tile([P, P], BF16, name="ident_bf16")
         masks.make_identity(nc, ident_bf16[:])
 
+        table_load = keep.tile([P, 1], F32, name="table_load")
+        nc.scalar.activation(out=table_load[:], in_=ones[:, 0:1], func=TANH)
+
         pair_rows = distance_matrix.rearrange("b i j k -> (b i) j k")
         dist = {}
         df_words = {}
 
-        def load_distances(n):
-            j, c = batch_of(n)
-            dist[n] = keep.tile([P, CHUNK_K], BF16, name="dist_%d" % n)
-            nc.sync.dma_start(out=dist[n][:], in_=pair_rows[:, j, c * CHUNK_K : (c + 1) * CHUNK_K])
+        def load_distances(u, count):
+            j, c = unit_of(u)
+            block = keep.tile([P, count * UNIT_K], BF16, name="dist_%d" % u)
+            nc.sync.dma_start(out=block[:], in_=pair_rows[:, j, c * UNIT_K : (c + count) * UNIT_K])
+            for s in range(count):
+                dist[u + s] = block[:, s * UNIT_K : (s + 1) * UNIT_K]
 
         def load_df_words(c):
-            df_words[c] = keep.tile([P, CHUNK_GROUPS, NH], U32, name="df_words_%d" % c, align_bytes=64)
-            groups = W_df_words[c * CHUNK_GROUPS : (c + 1) * CHUNK_GROUPS]
+            df_words[c] = keep.tile([P, UNIT_GROUPS, NH], U32, name="df_words_%d" % c, align_bytes=64)
+            groups = W_df_words[c * UNIT_GROUPS : (c + 1) * UNIT_GROUPS]
             nc.sync.dma_start(
                 out=df_words[c][:].bitcast(I32),
                 in_=groups.rearrange("g p n t -> p g (n t)").bitcast(I32),
             )
 
-        def load_df_scales(chunks):
-            for chunk in chunks:
-                for quadrant in range(4):
-                    nc.sync.dma_start(
-                        out=df_planes[32 * quadrant : 32 * quadrant + 16, chunk, :].bitcast(I32),
-                        in_=W_df_scales[
-                            chunk * CHUNK_GROUPS : (chunk + 1) * CHUNK_GROUPS, 4 * quadrant : 4 * quadrant + 4, :
-                        ].bitcast(I32),
-                    )
+        def load_df_scales(r, quadrant):
+            nc.sync.dma_start(
+                out=df_planes[32 * quadrant : 32 * quadrant + 16, r, :].bitcast(I32),
+                in_=W_df_scales[
+                    r * PLANE_GROUPS : (r + 1) * PLANE_GROUPS, 4 * quadrant : 4 * quadrant + 4, :
+                ].bitcast(I32),
+            )
 
-        load_distances(0)
-        load_distances(1)
-        for c in range(CHUNKS):
-            if c == 0:
-                load_df_scales([0])
-            load_df_words(c)
-            for n in range(FIRST_TILES * c + 2, FIRST_TILES * (c + 1) + 2):
-                if n < FIRST_TILES * CHUNKS:
-                    load_distances(n)
-            if c == 0:
-                load_df_scales(range(1, CHUNKS))
         atoms = keep.tile([P, NF], BF16, name="atoms")
-        nc.sync.dma_start(out=atoms[:], in_=atom_features.flatten_outer_dims())
         cf_rows = keep.tile([P, NF_TILES, NH], BF16, name="cf_rows")
-        nc.sync.dma_start(out=cf_rows[:], in_=W_cf.rearrange("(c p) n -> p c n", p=P))
-        nc.sync.dma_start(out=rows[0:1, :], in_=b_df.unsqueeze(0))
         bcf = keep.tile([P, PACK], BF16, name="bcf")
-        nc.sync.dma_start(out=bcf[:], in_=b_cf.rearrange("(p t) -> p t", t=PACK))
         mask_bf16 = keep.tile([P, ATOMS], BF16, name="mask_bf16")
-        nc.sync.dma_start(out=mask_bf16[:], in_=distance_matrix_mask.rearrange("b i j -> (b i) j"))
         fc_words = keep.tile([P, NF], U32, name="fc_words", align_bytes=64)
-        nc.sync.dma_start(
-            out=fc_words[:].bitcast(I32), in_=W_fc_words[0].rearrange("p n t -> p (n t)").bitcast(I32)
-        )
-        for r in range(4):
+
+        def load_fc_scales(r):
             nc.sync.dma_start(out=fc_plane[r:P:32, :].bitcast(I32), in_=W_fc_scales[0, r:16:4, :].bitcast(I32))
-        for n in range(FIRST_TILES * CHUNKS, BATCHES):
-            load_distances(n)
+
+        small_loads = [[] for c in range(STRIPS + 2)]
+        for r in range(1, GROUPS // PLANE_GROUPS):
+            for quadrant in range(4):
+                small_loads[2 * r - 2].append(lambda r=r, quadrant=quadrant: load_df_scales(r, quadrant))
+        small_loads[1] = [
+            lambda: nc.sync.dma_start(out=rows[0:1, :], in_=b_df.unsqueeze(0)),
+            lambda: nc.sync.dma_start(out=bcf[:], in_=b_cf.rearrange("(p t) -> p t", t=PACK)),
+            lambda: nc.sync.dma_start(out=mask_bf16[:], in_=distance_matrix_mask.rearrange("b i j -> (b i) j")),
+            lambda: nc.sync.dma_start(out=atoms[:], in_=atom_features.flatten_outer_dims()),
+        ]
+        small_loads[3] = [lambda: nc.sync.dma_start(out=cf_rows[:], in_=W_cf.rearrange("(c p) n -> p c n", p=P))]
+        small_loads[STRIPS] = [
+            lambda: nc.sync.dma_start(
+                out=fc_words[:].bitcast(I32), in_=W_fc_words[0].rearrange("p n t -> p (n t)").bitcast(I32)
+            )
+        ]
+        small_loads[STRIPS + 1] = [lambda r=r: load_fc_scales(r) for r in range(4)]
+
+        load_distances(0, 1)
+        for quadrant in range(4):
+            load_df_scales(0, quadrant)
+        for c in range(STRIPS):
+            load_df_words(c)
+            for s in range(FIRST_TILES):
+                if s < len(small_loads[c]):
+                    small_loads[c][s]()
+                u = FIRST_TILES * c + 1 + s
+                if u < FIRST_UNITS:
+                    load_distances(u, 1)
+        for u in range(FIRST_UNITS, UNITS, LOAD_UNITS):
+            load_distances(u, LOAD_UNITS)
+            c = STRIPS + (u - FIRST_UNITS) // STRIPS
+            s = (u - FIRST_UNITS) % STRIPS // LOAD_UNITS
+            if c < len(small_loads) and s < len(small_loads[c]):
+                small_loads[c][s]()
 
         sorted_words = {}
         flipped = {}
@@ -156,31 +177,26 @@ def tile_dtnnstep_pa_k_kernel(
         quantised = {}
         sums = {}
 
-        def sort_batch(n):
-            sorted_words[n] = sorted_pool.tile([P, CHUNK_GROUPS, 2, P], F32, name="sorted_words")
+        def sort_unit(u):
+            sorted_words[u] = sorted_pool.tile([P, UNIT_GROUPS, 2, P], F32, name="sorted_words")
             nc.vector.tensor_copy(
-                out=sorted_words[n][:],
-                in_=dist[n][:].bitcast(F32).rearrange("p (g w h) -> p g h w", g=CHUNK_GROUPS, h=2),
+                out=sorted_words[u][:],
+                in_=dist[u].bitcast(F32).rearrange("p (g w h) -> p g h w", g=UNIT_GROUPS, h=2),
             )
 
         def transpose_unit(u):
-            n, part = divmod(u, BATCH_BANKS)
-            flipped[u] = word_banks.tile([P, BANK_GROUPS, 2, P], F32, name="bank")
-            for s in range(BANK_GROUPS):
+            flipped[u] = word_banks.tile([P, UNIT_GROUPS, 2, P], F32, name="bank")
+            for s in range(UNIT_GROUPS):
                 for half in range(2):
-                    nc.tensor.transpose(
-                        flipped[u][:, s, half, :],
-                        sorted_words[n][:, part * BANK_GROUPS + s, half, :],
-                        ident_f32[:],
-                    )
+                    nc.tensor.transpose(flipped[u][:, s, half, :], sorted_words[u][:, s, half, :], ident_f32[:])
 
         def regroup_unit(u):
-            grouped[u] = grouped_pool.tile([P, BANK_GROUPS, P, PACK], BF16, name="grouped", align_bytes=64)
+            grouped[u] = grouped_pool.tile([P, UNIT_GROUPS, P, PACK], BF16, name="grouped", align_bytes=64)
             nc.scalar.copy(out=grouped[u][:].bitcast(F32), in_=flipped[u][:].rearrange("p s h r -> p s r h"))
 
         def quantise_unit(u):
-            codes = operands.tile([P, BANK_GROUPS, P], U32, name="codes", align_bytes=64)
-            scales = operands.tile([P, BANK_GROUPS, P], U8, name="scales", align_bytes=64)
+            codes = operands.tile([P, UNIT_GROUPS, P], U32, name="codes", align_bytes=64)
+            scales = operands.tile([P, UNIT_GROUPS, P], U8, name="scales", align_bytes=64)
             nc.vector.quantize_mx(
                 out=codes[:].rearrange("p s r -> p (s r)").bitcast(FP8X4),
                 scales=scales[:].rearrange("p s r -> p (s r)"),
@@ -189,23 +205,20 @@ def tile_dtnnstep_pa_k_kernel(
             quantised[u] = (codes, scales)
 
         def multiply_unit(u):
-            n, part = divmod(u, BATCH_BANKS)
-            j, c = batch_of(n)
+            j, c = unit_of(u)
             codes, scales = quantised[u]
-            if c == 0 and part == 0:
-                sums[j] = banks.tile(
-                    [P, NH], F32, name="bank_%d" % (j if j < FIRST_TILES else (j - FIRST_TILES) % 2)
-                )
-            for s in range(BANK_GROUPS):
-                g = part * BANK_GROUPS + s
+            if c == 0:
+                sums[j] = banks.tile([P, NH], F32, name="bank_%d" % (j if j < FIRST_TILES else j % 2))
+            for s in range(UNIT_GROUPS):
+                r, o = divmod(c * UNIT_GROUPS + s, PLANE_GROUPS)
                 nc.tensor.matmul_mx(
                     out=sums[j][:],
                     lhsT=codes[:, s, :].bitcast(FP8X4),
                     lhsT_scale=scales[:, s, :],
-                    rhs=df_words[c][:, g, :].bitcast(FP8X4),
-                    rhs_scale=df_planes[PACK * g : P, c, :],
-                    start=(c == 0 and g == 0),
-                    stop=(c == CHUNKS - 1 and g == CHUNK_GROUPS - 1),
+                    rhs=df_words[c][:, s, :].bitcast(FP8X4),
+                    rhs_scale=df_planes[PACK * o : P, r, :],
+                    start=(c == 0 and s == 0),
+                    stop=(c == STRIPS - 1 and s == UNIT_GROUPS - 1),
                 )
 
         bdf_all = keep.tile([P, PACK, P], BF16, name="bdf_all")
@@ -215,19 +228,19 @@ def tile_dtnnstep_pa_k_kernel(
         small = {}
 
         def spread_bias():
-            small["bias"] = banks.tile([P, BANK], F32, name="bank_flip")
+            small["bias"] = word_banks.tile([P, BANK], F32, name="bank")
             nc.tensor.matmul(out=small["bias"][:], lhsT=ones[:], rhs=rows[:], start=True, stop=True)
             nc.vector.tensor_copy(out=bdf_all[:], in_=small["bias"][:].rearrange("p (q t) -> p t q", t=PACK))
             nc.vector.tensor_copy(out=mask[:], in_=mask_bf16[:])
 
         def transpose_atoms():
-            flip = banks.tile([P, NF_TILES, P], BF16, name="bank_flip")
+            flip = word_banks.tile([P, NF_TILES, P], BF16, name="bank")
             for c in range(NF_TILES):
                 nc.tensor.transpose(flip[:, c, :], atoms[:, c * P : (c + 1) * P], ident_bf16[:])
             nc.scalar.copy(out=atoms_t[:], in_=flip[:])
 
         def atom_hidden():
-            product = banks.tile([P, PACK, P], F32, name="bank_flip")
+            product = word_banks.tile([P, PACK, P], F32, name="bank")
             for t in range(PACK):
                 for c in range(NF_TILES):
                     nc.tensor.matmul(
@@ -252,99 +265,125 @@ def tile_dtnnstep_pa_k_kernel(
         squashed = {}
         totals = {}
 
+        def parts(j):
+            return 2 if j == ROW_TILES - 1 else 1
+
         def add_bias(j):
-            biased[j] = work.tile([P, PACK, P], F32, name="biased")
-            nc.vector.tensor_tensor(
-                out=biased[j][:], in0=sums[j][:].rearrange("p (q t) -> p t q", t=PACK), in1=bdf_all[:], op=ADD
-            )
+            size = PACK // parts(j)
+            biased[j] = []
+            for first in range(0, PACK, size):
+                pool = biased_pool if size == PACK else work
+                piece = pool.tile([P, size, P], F32, name="biased_%d" % size)
+                nc.vector.tensor_tensor(
+                    out=piece[:],
+                    in0=sums[j][:].rearrange("p (q t) -> p t q", t=PACK)[:, first : first + size],
+                    in1=bdf_all[:, first : first + size],
+                    op=ADD,
+                )
+                biased[j].append(piece)
 
         def transpose_hidden(j):
-            hidden_t[j] = banks.tile([P, PACK, P], F32, name="bank_flip")
+            size = PACK // parts(j)
+            hidden_t[j] = banks.tile([P, PACK, P], F32, name="bank_2")
             for t in range(PACK):
-                nc.tensor.transpose(hidden_t[j][:, t, :], biased[j][:, t, :], ident_f32[:])
+                nc.tensor.transpose(hidden_t[j][:, t, :], biased[j][t // size][:, t % size, :], ident_f32[:])
 
         def gate(j):
+            size = MOLS // parts(j)
             gated[j] = work.tile([P, MOLS, ATOMS, PACK], BF16, name="gated", align_bytes=64)
-            nc.vector.tensor_tensor(
-                out=gated[j][:],
-                in0=hidden_t[j][:].rearrange("p t (b i) -> p b i t", i=ATOMS),
-                in1=atom_h[:, j].unsqueeze(2).to_broadcast([P, MOLS, ATOMS, PACK]),
-                op=MULT,
-            )
+            for first in range(0, MOLS, size):
+                nc.vector.tensor_tensor(
+                    out=gated[j][:, first : first + size],
+                    in0=hidden_t[j][:].rearrange("p t (b i) -> p b i t", i=ATOMS)[:, first : first + size],
+                    in1=atom_h[:, j, first : first + size].unsqueeze(2).to_broadcast([P, size, ATOMS, PACK]),
+                    op=MULT,
+                )
 
         def quantise_gated(j):
+            size = P // parts(j)
             codes = work.tile([P, P], U32, name="gated_codes", align_bytes=64)
             scales = work.tile([P, P], U8, name="gated_scales", align_bytes=64)
-            nc.vector.quantize_mx(
-                out=codes[:].bitcast(FP8X4), scales=scales[:], in_=gated[j][:].rearrange("p b i t -> p (b i t)")
-            )
+            columns = gated[j][:].rearrange("p b i t -> p (b i t)")
+            for first in range(0, P, size):
+                nc.vector.quantize_mx(
+                    out=codes[:, first : first + size].bitcast(FP8X4),
+                    scales=scales[:, first : first + size],
+                    in_=columns[:, first * PACK : (first + size) * PACK],
+                )
             gated_mx[j] = (codes, scales)
 
         def multiply_gated(j):
+            size = NF // parts(j)
             codes, scales = gated_mx[j]
-            products[j] = banks.tile([P, NF], F32, name="bank_2")
-            nc.tensor.matmul_mx(
-                out=products[j][:],
-                lhsT=codes[:].bitcast(FP8X4),
-                lhsT_scale=scales[:],
-                rhs=fc_words[:].bitcast(FP8X4),
-                rhs_scale=fc_plane[:],
-                start=True,
-                stop=True,
-            )
+            products[j] = []
+            for first in range(0, NF, size):
+                piece = banks.tile([P, size], F32, name="bank_3" if first == 0 else "bank_0")
+                nc.tensor.matmul_mx(
+                    out=piece[:],
+                    lhsT=codes[:].bitcast(FP8X4),
+                    lhsT_scale=scales[:],
+                    rhs=fc_words[:, first : first + size].bitcast(FP8X4),
+                    rhs_scale=fc_plane[:, first : first + size],
+                    start=True,
+                    stop=True,
+                )
+                products[j].append(piece)
 
         def squash(j):
-            squashed[j] = work.tile([P, NF], F32, name="squashed")
-            nc.scalar.activation(out=squashed[j][:], in_=products[j][:], func=TANH, scale=mask[:, j : j + 1])
+            squashed[j] = []
+            size = NF // parts(j)
+            for product in products[j]:
+                piece = work.tile([P, size], F32, name="squashed_%d" % size)
+                nc.scalar.activation(out=piece[:], in_=product[:], func=TANH, scale=mask[:, j : j + 1])
+                squashed[j].append(piece)
 
         def accumulate(j):
-            previous = atoms if j == 0 else totals[j - 1]
-            totals[j] = work.tile([P, NF], F32, name="total")
-            nc.vector.tensor_tensor(out=totals[j][:], in0=squashed[j][:], in1=previous[:], op=ADD)
+            size = NF // parts(j)
+            previous = atoms if j == 0 else totals[j - 1][0]
+            totals[j] = []
+            for piece in squashed[j]:
+                first = size * len(totals[j])
+                total = work.tile([P, size], F32, name="total_%d" % size)
+                nc.vector.tensor_tensor(out=total[:], in0=piece[:], in1=previous[:, first : first + size], op=ADD)
+                totals[j].append(total)
 
         rounds = rounds_of_units()
-        SMALL_ROUND = 7
         stage = {}
         start = 0
         for m in range(len(rounds)):
             for u in rounds[m]:
-                n, part = divmod(u, BATCH_BANKS)
-                j, c = batch_of(n)
-                if c == CHUNKS - 1 and part == BATCH_BANKS - 1:
+                j, c = unit_of(u)
+                if c == STRIPS - 1:
+                    stage.setdefault((0, m + 2), []).append(j)
                     start = max(start + 1, m + 2)
-                    for s in range(5):
-                        stage[(s, start + s)] = j
-        assert stage[(0, SMALL_ROUND + 2)] == 0
+                    for s in range(1, 5):
+                        stage.setdefault((s, start + s), []).append(j)
 
-        def sort_round(m):
-            if m < len(rounds):
-                for u in rounds[m]:
-                    if u % BATCH_BANKS == 0:
-                        sort_batch(u // BATCH_BANKS)
-
-        sort_round(0)
+        for u in rounds[0]:
+            sort_unit(u)
         for m in range(start + 5):
             fresh = rounds[m] if m < len(rounds) else []
             ripe = rounds[m - 1] if 0 <= m - 1 < len(rounds) else []
-            sort_round(m + 1)
-            if (0, m) in stage:
-                add_bias(stage[(0, m)])
-            if (2, m) in stage:
-                quantise_gated(stage[(2, m)])
-            if (3, m) in stage:
-                squash(stage[(3, m)])
-            if (4, m) in stage:
-                accumulate(stage[(4, m)])
+            for j in stage.get((0, m), []):
+                add_bias(j)
+            for u in rounds[m + 1] if m + 1 < len(rounds) else []:
+                sort_unit(u)
+            for j in stage.get((2, m), []):
+                quantise_gated(j)
+            for j in stage.get((3, m), []):
+                squash(j)
+            for j in stage.get((4, m), []):
+                accumulate(j)
             for u in fresh:
                 transpose_unit(u)
-            if (1, m) in stage:
-                transpose_hidden(stage[(1, m)])
+            for j in stage.get((1, m), []):
+                transpose_hidden(j)
             if m == SMALL_ROUND + 1:
                 transpose_atoms()
             for u in ripe:
                 multiply_unit(u)
-            if (2, m) in stage:
-                multiply_gated(stage[(2, m)])
+            for j in stage.get((2, m), []):
+                multiply_gated(j)
             if m == SMALL_ROUND:
                 spread_bias()
             if m == SMALL_ROUND + 2:
@@ -352,7 +391,10 @@ def tile_dtnnstep_pa_k_kernel(
             for u in fresh:
                 regroup_unit(u)
                 quantise_unit(u)
-            if (1, m) in stage:
-                gate(stage[(1, m)])
+            for j in stage.get((1, m), []):
+                gate(j)
 
-        nc.sync.dma_start(out=out.flatten_outer_dims(), in_=totals[ROW_TILES - 1][:])
+        first = 0
+        for size, piece in [(NF // parts(ROW_TILES - 1), piece) for piece in totals[ROW_TILES - 1]]:
+            nc.sync.dma_start(out=out.flatten_outer_dims()[:, first : first + size], in_=piece[:])
+            first += size

@@ -30,7 +30,8 @@ UNITS = ROW_TILES * STRIPS
 FIRST_UNITS = FIRST_TILES * STRIPS
 LOAD_UNITS = 2
 WORD_BANKS = 4
-FIRST_ROUNDS = 4
+LEAD = 4
+FIRST_ROUNDS = 1
 RUN = 3
 SMALL_ROUND = 10
 NF_TILES = NF // P
@@ -47,14 +48,28 @@ def unit_of(u):
     return j, c
 
 
-def rounds_of_units():
+def plan():
     rounds = []
+    stage = {}
     first = 0
-    while first < UNITS:
-        size = 1 if len(rounds) < FIRST_ROUNDS else RUN
+    start = 0
+    while first < UNITS or len(rounds) <= start + 4:
+        m = len(rounds)
+        size = RUN
+        if m < FIRST_ROUNDS:
+            size = 1
+        elif (1, m) in stage or m == SMALL_ROUND + 1:
+            size = RUN - 1
         rounds.append(list(range(first, min(first + size, UNITS))))
-        first += size
-    return rounds
+        first = min(first + size, UNITS)
+        for u in rounds[m]:
+            j, c = unit_of(u)
+            if c == STRIPS - 1:
+                stage.setdefault((0, m + 2), []).append(j)
+                start = max(start + 1, m + 2)
+                for s in range(1, 5):
+                    stage.setdefault((s, start + s), []).append(j)
+    return rounds, stage
 
 
 def tile_dtnnstep_pa_k_kernel(
@@ -153,7 +168,8 @@ def tile_dtnnstep_pa_k_kernel(
         ]
         small_loads[STRIPS + 1] = [lambda r=r: load_fc_scales(r) for r in range(4)]
 
-        load_distances(0, 1)
+        for u in range(LEAD):
+            load_distances(u, 1)
         for quadrant in range(4):
             load_df_scales(0, quadrant)
         for c in range(STRIPS):
@@ -161,7 +177,7 @@ def tile_dtnnstep_pa_k_kernel(
             for s in range(FIRST_TILES):
                 if s < len(small_loads[c]):
                     small_loads[c][s]()
-                u = FIRST_TILES * c + 1 + s
+                u = FIRST_TILES * c + LEAD + s
                 if u < FIRST_UNITS:
                     load_distances(u, 1)
         for u in range(FIRST_UNITS, UNITS, LOAD_UNITS):
@@ -284,7 +300,7 @@ def tile_dtnnstep_pa_k_kernel(
 
         def transpose_hidden(j):
             size = PACK // parts(j)
-            hidden_t[j] = banks.tile([P, PACK, P], F32, name="bank_2")
+            hidden_t[j] = word_banks.tile([P, PACK, P], F32, name="bank")
             for t in range(PACK):
                 nc.tensor.transpose(hidden_t[j][:, t, :], biased[j][t // size][:, t % size, :], ident_f32[:])
 
@@ -347,29 +363,18 @@ def tile_dtnnstep_pa_k_kernel(
                 nc.vector.tensor_tensor(out=total[:], in0=piece[:], in1=previous[:, first : first + size], op=ADD)
                 totals[j].append(total)
 
-        rounds = rounds_of_units()
-        stage = {}
-        start = 0
-        for m in range(len(rounds)):
-            for u in rounds[m]:
-                j, c = unit_of(u)
-                if c == STRIPS - 1:
-                    stage.setdefault((0, m + 2), []).append(j)
-                    start = max(start + 1, m + 2)
-                    for s in range(1, 5):
-                        stage.setdefault((s, start + s), []).append(j)
-
+        rounds, stage = plan()
         for u in rounds[0]:
             sort_unit(u)
-        for m in range(start + 5):
-            fresh = rounds[m] if m < len(rounds) else []
-            ripe = rounds[m - 1] if 0 <= m - 1 < len(rounds) else []
+        for m in range(len(rounds)):
+            fresh = rounds[m]
+            ripe = rounds[m - 1] if m > 0 else []
+            for j in stage.get((2, m), []):
+                quantise_gated(j)
             for j in stage.get((0, m), []):
                 add_bias(j)
             for u in rounds[m + 1] if m + 1 < len(rounds) else []:
                 sort_unit(u)
-            for j in stage.get((2, m), []):
-                quantise_gated(j)
             for j in stage.get((3, m), []):
                 squash(j)
             for j in stage.get((4, m), []):
@@ -390,9 +395,10 @@ def tile_dtnnstep_pa_k_kernel(
                 atom_hidden()
             for u in fresh:
                 regroup_unit(u)
-                quantise_unit(u)
             for j in stage.get((1, m), []):
                 gate(j)
+            for u in fresh:
+                quantise_unit(u)
 
         first = 0
         for size, piece in [(NF // parts(ROW_TILES - 1), piece) for piece in totals[ROW_TILES - 1]]:

@@ -98,8 +98,8 @@ def tile_dtnnstep_pa_k_kernel(
         word_banks = stack.enter_context(tc.psum_pool(name="word_banks", bufs=WORD_BANKS))
         stack.enter_context(tc.manual_schedule())
 
-        df_planes = keep.tile([P, GROUPS // PLANE_GROUPS, NH], U8, name="df_planes", align_bytes=64)
-        fc_plane = keep.tile([P, NF], U8, name="fc_plane", align_bytes=64)
+        df_planes = keep.tile([P, GROUPS // PLANE_GROUPS, NH], U8, name="df_planes", align_bytes=256)
+        fc_plane = keep.tile([P, NF], U8, name="fc_plane", align_bytes=256)
         nc.vector.memset(df_planes[:].bitcast(I32), 0)
         nc.vector.memset(fc_plane[:].bitcast(I32), 0)
         rows = keep.tile([P, NH], BF16, name="rows")
@@ -126,7 +126,7 @@ def tile_dtnnstep_pa_k_kernel(
                 dist[u + s] = block[:, s * UNIT_K : (s + 1) * UNIT_K]
 
         def load_df_words(c):
-            df_words[c] = keep.tile([P, UNIT_GROUPS, NH], U32, name="df_words_%d" % c, align_bytes=64)
+            df_words[c] = keep.tile([P, UNIT_GROUPS, NH], U32, name="df_words_%d" % c, align_bytes=256)
             groups = W_df_words[c * UNIT_GROUPS : (c + 1) * UNIT_GROUPS]
             nc.sync.dma_start(
                 out=df_words[c][:].bitcast(I32),
@@ -145,7 +145,7 @@ def tile_dtnnstep_pa_k_kernel(
         cf_rows = keep.tile([P, NF_TILES, NH], BF16, name="cf_rows")
         bcf = keep.tile([P, PACK], BF16, name="bcf")
         mask_bf16 = keep.tile([P, ATOMS], BF16, name="mask_bf16")
-        fc_words = keep.tile([P, NF], U32, name="fc_words", align_bytes=64)
+        fc_words = keep.tile([P, NF], U32, name="fc_words", align_bytes=256)
 
         def load_fc_scales(r):
             nc.sync.dma_start(out=fc_plane[r:P:32, :].bitcast(I32), in_=W_fc_scales[0, r:16:4, :].bitcast(I32))
@@ -207,12 +207,12 @@ def tile_dtnnstep_pa_k_kernel(
                     nc.tensor.transpose(flipped[u][:, s, half, :], sorted_words[u][:, s, half, :], ident_f32[:])
 
         def regroup_unit(u):
-            grouped[u] = grouped_pool.tile([P, UNIT_GROUPS, P, PACK], BF16, name="grouped", align_bytes=64)
+            grouped[u] = grouped_pool.tile([P, UNIT_GROUPS, P, PACK], BF16, name="grouped", align_bytes=256)
             nc.scalar.copy(out=grouped[u][:].bitcast(F32), in_=flipped[u][:].rearrange("p s h r -> p s r h"))
 
         def quantise_unit(u):
-            codes = operands.tile([P, UNIT_GROUPS, P], U32, name="codes", align_bytes=64)
-            scales = operands.tile([P, UNIT_GROUPS, P], U8, name="scales", align_bytes=64)
+            codes = operands.tile([P, UNIT_GROUPS, P], U32, name="codes", align_bytes=256)
+            scales = operands.tile([P, UNIT_GROUPS, P], U8, name="scales", align_bytes=256)
             nc.vector.quantize_mx(
                 out=codes[:].rearrange("p s r -> p (s r)").bitcast(FP8X4),
                 scales=scales[:].rearrange("p s r -> p (s r)"),
@@ -306,7 +306,7 @@ def tile_dtnnstep_pa_k_kernel(
 
         def gate(j):
             size = MOLS // parts(j)
-            gated[j] = work.tile([P, MOLS, ATOMS, PACK], BF16, name="gated", align_bytes=64)
+            gated[j] = work.tile([P, MOLS, ATOMS, PACK], BF16, name="gated", align_bytes=256)
             for first in range(0, MOLS, size):
                 nc.vector.tensor_tensor(
                     out=gated[j][:, first : first + size],
@@ -317,8 +317,8 @@ def tile_dtnnstep_pa_k_kernel(
 
         def quantise_gated(j):
             size = P // parts(j)
-            codes = work.tile([P, P], U32, name="gated_codes", align_bytes=64)
-            scales = work.tile([P, P], U8, name="gated_scales", align_bytes=64)
+            codes = work.tile([P, P], U32, name="gated_codes", align_bytes=256)
+            scales = work.tile([P, P], U8, name="gated_scales", align_bytes=256)
             columns = gated[j][:].rearrange("p b i t -> p (b i t)")
             for first in range(0, P, size):
                 nc.vector.quantize_mx(

from contextlib import ExitStack

import concourse.masks as masks
import concourse.mybir as mybir

F32 = mybir.dt.float32
BF16 = mybir.dt.bfloat16
I32 = mybir.dt.int32
U32 = mybir.dt.uint32
U8 = mybir.dt.uint8
FP8X4 = mybir.dt.float8_e4m3fn_x4
ADD = mybir.AluOpType.add
MULT = mybir.AluOpType.mult
TANH = mybir.ActivationFunctionType.Tanh

P = 128
PACK = 4
K_PASS = P * PACK
BANK = 512
MOLS, ATOMS = 16, 8
NF, ND, NH = 512, 8192, 512
GROUPS = ND // K_PASS
ROW_TILES = ATOMS
FIRST_TILES = 4
PLANE_GROUPS = 4
UNIT_GROUPS = 2
UNIT_K = UNIT_GROUPS * K_PASS
STRIPS = GROUPS // UNIT_GROUPS
UNITS = ROW_TILES * STRIPS
FIRST_UNITS = FIRST_TILES * STRIPS
LOAD_UNITS = 2
WORD_BANKS = 4
LEAD = 4
FIRST_ROUNDS = 1
RUN = 3
SMALL_ROUND = 10
NF_TILES = NF // P
PAIRS_OF_ATOMS = MOLS * ATOMS * ATOMS

FLOPS = 2 * PAIRS_OF_ATOMS * ND * NH + 2 * MOLS * ATOMS * NF * NH + 2 * PAIRS_OF_ATOMS * NH * NF


def unit_of(u):
    if u < FIRST_UNITS:
        c, j = divmod(u, FIRST_TILES)
    else:
        j, c = divmod(u, STRIPS)
    return j, c


def plan():
    rounds = []
    stage = {}
    first = 0
    start = 0
    while first < UNITS or len(rounds) <= start + 4:
        m = len(rounds)
        size = RUN
        if m < FIRST_ROUNDS:
            size = 1
        elif (1, m) in stage or m == SMALL_ROUND + 1:
            size = RUN - 1
        rounds.append(list(range(first, min(first + size, UNITS))))
        first = min(first + size, UNITS)
        for u in rounds[m]:
            j, c = unit_of(u)
            if c == STRIPS - 1:
                stage.setdefault((0, m + 2), []).append(j)
                start = max(start + 1, m + 2)
                for s in range(1, 5):
                    stage.setdefault((s, start + s), []).append(j)
    return rounds, stage


def tile_dtnnstep_pa_k_kernel(
    tc,
    atom_features,
    distance_matrix,
    distance_matrix_mask,
    W_cf,
    W_df_words,
    W_df_scales,
    W_fc_words,
    W_fc_scales,
    b_cf,
    b_df,
    out,
):
    nc = tc.nc
    with ExitStack() as stack:
        keep = stack.enter_context(tc.tile_pool(name="keep", bufs=1))
        work = stack.enter_context(tc.tile_pool(name="work", bufs=2))
        operands = stack.enter_context(tc.tile_pool(name="operands", bufs=2 * RUN + 2))
        sorted_pool = stack.enter_context(tc.tile_pool(name="sorted_pool", bufs=2 * RUN + 2))
        biased_pool = stack.enter_context(tc.tile_pool(name="biased_pool", bufs=FIRST_TILES))
        grouped_pool = stack.enter_context(tc.tile_pool(name="grouped_pool", bufs=WORD_BANKS))
        banks = stack.enter_context(tc.psum_pool(name="banks", bufs=1))
        word_banks = stack.enter_context(tc.psum_pool(name="word_banks", bufs=WORD_BANKS))
        stack.enter_context(tc.manual_schedule())

        df_planes = keep.tile([P, GROUPS // PLANE_GROUPS, NH], U8, name="df_planes", align_bytes=256)
        fc_plane = keep.tile([P, NF], U8, name="fc_plane", align_bytes=256)
        nc.vector.memset(df_planes[:].bitcast(I32), 0)
        nc.vector.memset(fc_plane[:].bitcast(I32), 0)
        rows = keep.tile([P, NH], BF16, name="rows")
        nc.vector.memset(rows[:].bitcast(I32), 0)
        ones = keep.tile([P, P], BF16, name="ones")
        nc.vector.memset(ones[:], 1.0)
        ident_f32 = keep.tile([P, P], F32, name="ident_f32")
        masks.make_identity(nc, ident_f32[:])
        ident_bf16 = keep.tile([P, P], BF16, name="ident_bf16")
        masks.make_identity(nc, ident_bf16[:])

        table_load = keep.tile([P, 1], F32, name="table_load")
        nc.scalar.activation(out=table_load[:], in_=ones[:, 0:1], func=TANH)

        pair_rows = distance_matrix.rearrange("b i j k -> (b i) j k")
        dist = {}
        df_words = {}

        def load_distances(u, count):
            j, c = unit_of(u)
            block = keep.tile([P, count * UNIT_K], BF16, name="dist_%d" % u)
            nc.sync.dma_start(out=block[:], in_=pair_rows[:, j, c * UNIT_K : (c + count) * UNIT_K])
            for s in range(count):
                dist[u + s] = block[:, s * UNIT_K : (s + 1) * UNIT_K]

        def load_df_words(c):
            df_words[c] = keep.tile([P, UNIT_GROUPS, NH], U32, name="df_words_%d" % c, align_bytes=256)
            groups = W_df_words[c * UNIT_GROUPS : (c + 1) * UNIT_GROUPS]
            nc.sync.dma_start(
                out=df_words[c][:].bitcast(I32),
                in_=groups.rearrange("g p n t -> p g (n t)").bitcast(I32),
            )

        def load_df_scales(r, quadrant):
            nc.sync.dma_start(
                out=df_planes[32 * quadrant : 32 * quadrant + 16, r, :].bitcast(I32),
                in_=W_df_scales[
                    r * PLANE_GROUPS : (r + 1) * PLANE_GROUPS, 4 * quadrant : 4 * quadrant + 4, :
                ].bitcast(I32),
            )

        atoms = keep.tile([P, NF], BF16, name="atoms")
        cf_rows = keep.tile([P, NF_TILES, NH], BF16, name="cf_rows")
        bcf = keep.tile([P, PACK], BF16, name="bcf")
        mask_bf16 = keep.tile([P, ATOMS], BF16, name="mask_bf16")
        fc_words = keep.tile([P, NF], U32, name="fc_words", align_bytes=256)

        def load_fc_scales(r):
            nc.sync.dma_start(out=fc_plane[r:P:32, :].bitcast(I32), in_=W_fc_scales[0, r:16:4, :].bitcast(I32))

        small_loads = [[] for c in range(STRIPS + 2)]
        for r in range(1, GROUPS // PLANE_GROUPS):
            for quadrant in range(4):
                small_loads[2 * r - 2].append(lambda r=r, quadrant=quadrant: load_df_scales(r, quadrant))
        small_loads[1] = [
            lambda: nc.sync.dma_start(out=rows[0:1, :], in_=b_df.unsqueeze(0)),
            lambda: nc.sync.dma_start(out=bcf[:], in_=b_cf.rearrange("(p t) -> p t", t=PACK)),
            lambda: nc.sync.dma_start(out=mask_bf16[:], in_=distance_matrix_mask.rearrange("b i j -> (b i) j")),
            lambda: nc.sync.dma_start(out=atoms[:], in_=atom_features.flatten_outer_dims()),
        ]
        small_loads[3] = [lambda: nc.sync.dma_start(out=cf_rows[:], in_=W_cf.rearrange("(c p) n -> p c n", p=P))]
        small_loads[STRIPS] = [
            lambda: nc.sync.dma_start(
                out=fc_words[:].bitcast(I32), in_=W_fc_words[0].rearrange("p n t -> p (n t)").bitcast(I32)
            )
        ]
        small_loads[STRIPS + 1] = [lambda r=r: load_fc_scales(r) for r in range(4)]

        for u in range(LEAD):
            load_distances(u, 1)
        for quadrant in range(4):
            load_df_scales(0, quadrant)
        for c in range(STRIPS):
            load_df_words(c)
            for s in range(FIRST_TILES):
                if s < len(small_loads[c]):
                    small_loads[c][s]()
                u = FIRST_TILES * c + LEAD + s
                if u < FIRST_UNITS:
                    load_distances(u, 1)
        for u in range(FIRST_UNITS, UNITS, LOAD_UNITS):
            load_distances(u, LOAD_UNITS)
            c = STRIPS + (u - FIRST_UNITS) // STRIPS
            s = (u - FIRST_UNITS) % STRIPS // LOAD_UNITS
            if c < len(small_loads) and s < len(small_loads[c]):
                small_loads[c][s]()

        sorted_words = {}
        flipped = {}
        grouped = {}
        quantised = {}
        sums = {}

        def sort_unit(u):
            sorted_words[u] = sorted_pool.tile([P, UNIT_GROUPS, 2, P], F32, name="sorted_words")
            nc.vector.tensor_copy(
                out=sorted_words[u][:],
                in_=dist[u].bitcast(F32).rearrange("p (g w h) -> p g h w", g=UNIT_GROUPS, h=2),
            )

        def transpose_unit(u):
            flipped[u] = word_banks.tile([P, UNIT_GROUPS, 2, P], F32, name="bank")
            for s in range(UNIT_GROUPS):
                for half in range(2):
                    nc.tensor.transpose(flipped[u][:, s, half, :], sorted_words[u][:, s, half, :], ident_f32[:])

        def regroup_unit(u):
            grouped[u] = grouped_pool.tile([P, UNIT_GROUPS, P, PACK], BF16, name="grouped", align_bytes=256)
            nc.scalar.copy(out=grouped[u][:].bitcast(F32), in_=flipped[u][:].rearrange("p s h r -> p s r h"))

        def quantise_unit(u):
            codes = operands.tile([P, UNIT_GROUPS, P], U32, name="codes", align_bytes=256)
            scales = operands.tile([P, UNIT_GROUPS, P], U8, name="scales", align_bytes=256)
            nc.vector.quantize_mx(
                out=codes[:].rearrange("p s r -> p (s r)").bitcast(FP8X4),
                scales=scales[:].rearrange("p s r -> p (s r)"),
                in_=grouped[u][:].rearrange("p s r t -> p (s r t)"),
            )
            quantised[u] = (codes, scales)

        def multiply_unit(u):
            j, c = unit_of(u)
            codes, scales = quantised[u]
            if c == 0:
                sums[j] = banks.tile([P, NH], F32, name="bank_%d" % (j if j < FIRST_TILES else j % 2))
            for s in range(UNIT_GROUPS):
                r, o = divmod(c * UNIT_GROUPS + s, PLANE_GROUPS)
                nc.tensor.matmul_mx(
                    out=sums[j][:],
                    lhsT=codes[:, s, :].bitcast(FP8X4),
                    lhsT_scale=scales[:, s, :],
                    rhs=df_words[c][:, s, :].bitcast(FP8X4),
                    rhs_scale=df_planes[PACK * o : P, r, :],
                    start=(c == 0 and s == 0),
                    stop=(c == STRIPS - 1 and s == UNIT_GROUPS - 1),
                )

        bdf_all = keep.tile([P, PACK, P], BF16, name="bdf_all")
        mask = keep.tile([P, ATOMS], F32, name="mask")
        atoms_t = keep.tile([P, NF_TILES, P], BF16, name="atoms_t")
        atom_h = keep.tile([P, ATOMS, MOLS, PACK], F32, name="atom_h")
        small = {}

        def spread_bias():
            small["bias"] = word_banks.tile([P, BANK], F32, name="bank")
            nc.tensor.matmul(out=small["bias"][:], lhsT=ones[:], rhs=rows[:], start=True, stop=True)
            nc.vector.tensor_copy(out=bdf_all[:], in_=small["bias"][:].rearrange("p (q t) -> p t q", t=PACK))
            nc.vector.tensor_copy(out=mask[:], in_=mask_bf16[:])

        def transpose_atoms():
            flip = word_banks.tile([P, NF_TILES, P], BF16, name="bank")
            for c in range(NF_TILES):
                nc.tensor.transpose(flip[:, c, :], atoms[:, c * P : (c + 1) * P], ident_bf16[:])
            nc.scalar.copy(out=atoms_t[:], in_=flip[:])

        def atom_hidden():
            product = word_banks.tile([P, PACK, P], F32, name="bank")
            for t in range(PACK):
                for c in range(NF_TILES):
                    nc.tensor.matmul(
                        out=product[:, t, :],
                        lhsT=cf_rows[:, c, t:NH:PACK],
                        rhs=atoms_t[:, c, :],
                        start=(c == 0),
                        stop=(c == NF_TILES - 1),
                    )
            nc.vector.tensor_tensor(
                out=atom_h[:],
                in0=product[:].rearrange("p t (b j) -> p j b t", j=ATOMS),
                in1=bcf[:].unsqueeze(1).unsqueeze(1).to_broadcast([P, ATOMS, MOLS, PACK]),
                op=ADD,
            )

        biased = {}
        hidden_t = {}
        gated = {}
        gated_mx = {}
        products = {}
        squashed = {}
        totals = {}

        def parts(j):
            return 2 if j == ROW_TILES - 1 else 1

        def add_bias(j):
            size = PACK // parts(j)
            biased[j] = []
            for first in range(0, PACK, size):
                pool = biased_pool if size == PACK else work
                piece = pool.tile([P, size, P], F32, name="biased_%d" % size)
                nc.vector.tensor_tensor(
                    out=piece[:],
                    in0=sums[j][:].rearrange("p (q t) -> p t q", t=PACK)[:, first : first + size],
                    in1=bdf_all[:, first : first + size],
                    op=ADD,
                )
                biased[j].append(piece)

        def transpose_hidden(j):
            size = PACK // parts(j)
            hidden_t[j] = word_banks.tile([P, PACK, P], F32, name="bank")
            for t in range(PACK):
                nc.tensor.transpose(hidden_t[j][:, t, :], biased[j][t // size][:, t % size, :], ident_f32[:])

        def gate(j):
            size = MOLS // parts(j)
            gated[j] = work.tile([P, MOLS, ATOMS, PACK], BF16, name="gated", align_bytes=256)
            for first in range(0, MOLS, size):
                nc.vector.tensor_tensor(
                    out=gated[j][:, first : first + size],
                    in0=hidden_t[j][:].rearrange("p t (b i) -> p b i t", i=ATOMS)[:, first : first + size],
                    in1=atom_h[:, j, first : first + size].unsqueeze(2).to_broadcast([P, size, ATOMS, PACK]),
                    op=MULT,
                )

        def quantise_gated(j):
            size = P // parts(j)
            codes = work.tile([P, P], U32, name="gated_codes", align_bytes=256)
            scales = work.tile([P, P], U8, name="gated_scales", align_bytes=256)
            columns = gated[j][:].rearrange("p b i t -> p (b i t)")
            for first in range(0, P, size):
                nc.vector.quantize_mx(
                    out=codes[:, first : first + size].bitcast(FP8X4),
                    scales=scales[:, first : first + size],
                    in_=columns[:, first * PACK : (first + size) * PACK],
                )
            gated_mx[j] = (codes, scales)

        def multiply_gated(j):
            size = NF // parts(j)
            codes, scales = gated_mx[j]
            products[j] = []
            for first in range(0, NF, size):
                piece = banks.tile([P, size], F32, name="bank_3" if first == 0 else "bank_0")
                nc.tensor.matmul_mx(
                    out=piece[:],
                    lhsT=codes[:].bitcast(FP8X4),
                    lhsT_scale=scales[:],
                    rhs=fc_words[:, first : first + size].bitcast(FP8X4),
                    rhs_scale=fc_plane[:, first : first + size],
                    start=True,
                    stop=True,
                )
                products[j].append(piece)

        def squash(j):
            squashed[j] = []
            size = NF // parts(j)
            for product in products[j]:
                piece = work.tile([P, size], F32, name="squashed_%d" % size)
                nc.scalar.activation(out=piece[:], in_=product[:], func=TANH, scale=mask[:, j : j + 1])
                squashed[j].append(piece)

        def accumulate(j):
            size = NF // parts(j)
            previous = atoms if j == 0 else totals[j - 1][0]
            totals[j] = []
            for piece in squashed[j]:
                first = size * len(totals[j])
                total = work.tile([P, size], F32, name="total_%d" % size)
                nc.vector.tensor_tensor(out=total[:], in0=piece[:], in1=previous[:, first : first + size], op=ADD)
                totals[j].append(total)

        rounds, stage = plan()
        for u in rounds[0]:
            sort_unit(u)
        for m in range(len(rounds)):
            fresh = rounds[m]
            ripe = rounds[m - 1] if m > 0 else []
            for j in stage.get((2, m), []):
                quantise_gated(j)
            for j in stage.get((0, m), []):
                add_bias(j)
            for u in rounds[m + 1] if m + 1 < len(rounds) else []:
                sort_unit(u)
            for j in stage.get((3, m), []):
                squash(j)
            for j in stage.get((4, m), []):
                accumulate(j)
            for u in fresh:
                transpose_unit(u)
            for j in stage.get((1, m), []):
                transpose_hidden(j)
            if m == SMALL_ROUND + 1:
                transpose_atoms()
            for u in ripe:
                multiply_unit(u)
            for j in stage.get((2, m), []):
                multiply_gated(j)
            if m == SMALL_ROUND:
                spread_bias()
            if m == SMALL_ROUND + 2:
                atom_hidden()
            for u in fresh:
                regroup_unit(u)
            for j in stage.get((1, m), []):
                gate(j)
            for u in fresh:
                quantise_unit(u)

        first = 0
        for size, piece in [(NF // parts(ROW_TILES - 1), piece) for piece in totals[ROW_TILES - 1]]:
            nc.sync.dma_start(out=out.flatten_outer_dims()[:, first : first + size], in_=piece[:])
            first += size
